import numpy as np
import ml_dtypes

BF16 = ml_dtypes.bfloat16


def bf(x):
    return np.asarray(x, np.float32).astype(BF16)


def f32(x):
    return np.asarray(x, np.float32)


def f64(x):
    return np.asarray(x).astype(np.float64)


def striped(idx):
    return np.tile(idx.reshape(-1, 16).T, (8, 1))


C, S, K, D, Q, N, HALF, RUNS = 128, 1024, 4, 2, 4, 8192, 512, 16


def sigmoid(v):
    return 1.0 / (1.0 + np.exp(-v))


def setup_inputs():
    h = f32(np.random.standard_normal((C, S)))
    cell = f32(np.random.standard_normal((C, S)))
    mask = f32(np.tile(np.random.uniform(size=(1, N)), (C, 1)))
    w = bf(np.random.standard_normal((D * C, Q * C)) / np.sqrt(C))
    u = bf(np.random.standard_normal((C, Q * C)) / np.sqrt(C))
    b = f32(0.1 * np.random.standard_normal((Q * C, 1)))
    idx = np.concatenate([np.random.permutation(S)[:HALF] for _ in range(RUNS)])
    return {"h": h, "cell": cell, "mask": mask, "w": w, "u": u, "b": b, "offs": striped(idx)}


def reference(h, cell, mask, w, u, b, offs):
    idx = offs[:16].T.reshape(-1)
    msg = f64(h)[:, idx] * f64(mask)
    agg = msg.reshape(C, D, S, K).sum(axis=3)
    agg2 = agg.transpose(1, 0, 2).reshape(D * C, S)
    pre = f64(w).T @ agg2 + f64(u).T @ f64(h) + f64(b)
    pre = pre.reshape(Q, C, S)
    gate_i = sigmoid(pre[0])
    gate_o = sigmoid(pre[1])
    gate_f = sigmoid(pre[2])
    cand = np.tanh(pre[3])
    cnew = gate_f * f64(cell) + gate_i * cand
    return gate_o * np.tanh(cnew)

@@ -1,0 +1,103 @@
+import concourse.mybir as mybir
+
+F32, BF16, U16 = mybir.dt.float32, mybir.dt.bfloat16, mybir.dt.uint16
+MULT, ADD = mybir.AluOpType.mult, mybir.AluOpType.add
+SIGMOID = mybir.ActivationFunctionType.Sigmoid
+TANH = mybir.ActivationFunctionType.Tanh
+
+C = 128
+S = 1024
+K = 4
+D = 2
+Q = 4
+N = D * S * K
+
+BLOCK = 256
+BLOCKS = S // BLOCK
+PIECE = BLOCK * K
+PIECE_COLS = PIECE // 16
+
+FLOPS = 2 * (D * C + C) * (Q * C) * S
+
+
+def tile_gslstm_kernel(tc, h, cell, mask, w, u, b, offs, out):
+    nc = tc.nc
+    with (
+        tc.tile_pool(name="held", bufs=1) as held,
+        tc.tile_pool(name="work", bufs=2) as work,
+        tc.psum_pool(name="psum", bufs=2) as psum,
+    ):
+        offsets = held.tile([C, N // 16], U16, name="offsets")
+        nc.sync.dma_start(offsets[:], offs)
+        h_f32 = held.tile([C, S], F32, name="h_f32")
+        nc.scalar.dma_start(h_f32[:], h)
+
+        mask_pieces = {}
+        for t in range(BLOCKS):
+            for d in range(D):
+                first = (d * S + t * BLOCK) * K
+                mask_pieces[d, t] = held.tile([C, PIECE], F32, name=f"mask_{d}_{t}")
+                nc.sync.dma_start(mask_pieces[d, t][:], mask[:, first : first + PIECE])
+
+        u_bf = held.tile([C, Q * C], BF16, name="u_bf")
+        nc.scalar.dma_start(u_bf[:], u)
+        w_bf = held.tile([C, D, Q * C], BF16, name="w_bf")
+        nc.scalar.dma_start(w_bf[:], w.rearrange("(d c) m -> c d m", d=D))
+        cell_f32 = held.tile([C, S], F32, name="cell_f32")
+        nc.scalar.dma_start(cell_f32[:], cell)
+        bias = held.tile([C, Q], F32, name="bias")
+        with nc.allow_non_contiguous_dma(reason="512 biases, one to a partition and gate"):
+            nc.scalar.dma_start(bias[:], b.rearrange("(q m) one -> m (q one)", q=Q))
+
+        h_bf = held.tile([C, S], BF16, name="h_bf")
+        nc.scalar.copy(h_bf[:], h_f32[:])
+
+        for t in range(BLOCKS):
+            nodes = slice(t * BLOCK, (t + 1) * BLOCK)
+
+            agg = {}
+            for d in range(D):
+                piece = d * BLOCKS + t
+                msg = work.tile([C, PIECE], F32, name="msg")
+                nc.vector.tensor_tensor(
+                    msg[:],
+                    h_f32[:].indirect(offsets[:, piece * PIECE_COLS : (piece + 1) * PIECE_COLS]),
+                    mask_pieces[d, t][:],
+                    MULT,
+                )
+                msg_pairs = msg[:].rearrange("c (j two) -> c j two", two=2)
+                half = work.tile([C, PIECE // 2], F32, name="half")
+                nc.vector.tensor_tensor(half[:], msg_pairs[:, :, 0], msg_pairs[:, :, 1], ADD)
+                half_pairs = half[:].rearrange("c (n two) -> c n two", two=2)
+                agg[d] = work.tile([C, BLOCK], BF16, name=f"agg{d}")
+                nc.vector.tensor_tensor(agg[d][:], half_pairs[:, :, 0], half_pairs[:, :, 1], ADD)
+
+            pre = [psum.tile([C, BLOCK], F32, name=f"pre{q}") for q in range(Q)]
+            for q in range(Q):
+                gate_cols = slice(q * C, (q + 1) * C)
+                nc.tensor.matmul(pre[q][:], u_bf[:, gate_cols], h_bf[:, nodes], start=True, stop=False)
+            for d in range(D):
+                for q in range(Q):
+                    gate_cols = slice(q * C, (q + 1) * C)
+                    nc.tensor.matmul(
+                        pre[q][:], w_bf[:, d, gate_cols], agg[d][:], start=False, stop=(d == D - 1)
+                    )
+
+            gate = []
+            for q in range(Q):
+                gate.append(work.tile([C, BLOCK], F32, name=f"gate{q}"))
+                nc.scalar.activation(
+                    gate[q][:], pre[q][:], TANH if q == Q - 1 else SIGMOID, bias=bias[:, q : q + 1]
+                )
+            gate_i, gate_o, gate_f, cand = gate
+            kept = work.tile([C, BLOCK], F32, name="kept")
+            nc.gpsimd.tensor_tensor(kept[:], gate_f[:], cell_f32[:, nodes], MULT)
+            fresh = work.tile([C, BLOCK], F32, name="fresh")
+            nc.gpsimd.tensor_tensor(fresh[:], gate_i[:], cand[:], MULT)
+            cnew = work.tile([C, BLOCK], F32, name="cnew")
+            nc.gpsimd.tensor_tensor(cnew[:], kept[:], fresh[:], ADD)
+            squashed = work.tile([C, BLOCK], F32, name="squashed")
+            nc.scalar.activation(squashed[:], cnew[:], TANH)
+            result = work.tile([C, BLOCK], F32, name="result")
+            nc.gpsimd.tensor_tensor(result[:], gate_o[:], squashed[:], MULT)
+            nc.sync.dma_start(out[:, nodes], result[:])

@@ -91,13 +91,13 @@ def tile_gslstm_kernel(tc, h, cell, mask, w, u, b, offs, out):
                 )
             gate_i, gate_o, gate_f, cand = gate
             kept = work.tile([C, BLOCK], F32, name="kept")
-            nc.gpsimd.tensor_tensor(kept[:], gate_f[:], cell_f32[:, nodes], MULT)
+            nc.vector.tensor_tensor(kept[:], gate_f[:], cell_f32[:, nodes], MULT)
             fresh = work.tile([C, BLOCK], F32, name="fresh")
-            nc.gpsimd.tensor_tensor(fresh[:], gate_i[:], cand[:], MULT)
+            nc.vector.tensor_tensor(fresh[:], gate_i[:], cand[:], MULT)
             cnew = work.tile([C, BLOCK], F32, name="cnew")
-            nc.gpsimd.tensor_tensor(cnew[:], kept[:], fresh[:], ADD)
+            nc.vector.tensor_tensor(cnew[:], kept[:], fresh[:], ADD)
             squashed = work.tile([C, BLOCK], F32, name="squashed")
             nc.scalar.activation(squashed[:], cnew[:], TANH)
             result = work.tile([C, BLOCK], F32, name="result")
-            nc.gpsimd.tensor_tensor(result[:], gate_o[:], squashed[:], MULT)
+            nc.vector.tensor_tensor(result[:], gate_o[:], squashed[:], MULT)
             nc.sync.dma_start(out[:, nodes], result[:])

@@ -1,4 +1,5 @@
 import concourse.mybir as mybir
+from concourse.masks import make_identity
 
 F32, BF16, U16 = mybir.dt.float32, mybir.dt.bfloat16, mybir.dt.uint16
 MULT, ADD = mybir.AluOpType.mult, mybir.AluOpType.add
@@ -9,6 +10,7 @@ C = 128
 S = 1024
 K = 4
 D = 2
+GATE_I, GATE_O, GATE_F, GATE_Z = 0, 1, 2, 3
 Q = 4
 N = D * S * K
 
@@ -16,6 +18,7 @@ BLOCK = 256
 BLOCKS = S // BLOCK
 PIECE = BLOCK * K
 PIECE_COLS = PIECE // 16
+LAG = 1
 
 FLOPS = 2 * (D * C + C) * (Q * C) * S
 
@@ -24,8 +27,10 @@ def tile_gslstm_kernel(tc, h, cell, mask, w, u, b, offs, out):
     nc = tc.nc
     with (
         tc.tile_pool(name="held", bufs=1) as held,
-        tc.tile_pool(name="work", bufs=2) as work,
-        tc.psum_pool(name="psum", bufs=2) as psum,
+        tc.tile_pool(name="work", bufs=3) as work,
+        tc.tile_pool(name="gates", bufs=LAG + 1) as gates,
+        tc.psum_pool(name="psum", bufs=1) as psum,
+        tc.psum_pool(name="psum_sums", bufs=2) as psum_sums,
     ):
         offsets = held.tile([C, N // 16], U16, name="offsets")
         nc.sync.dma_start(offsets[:], offs)
@@ -51,53 +56,77 @@ def tile_gslstm_kernel(tc, h, cell, mask, w, u, b, offs, out):
 
         h_bf = held.tile([C, S], BF16, name="h_bf")
         nc.scalar.copy(h_bf[:], h_f32[:])
+        identity = held.tile([C, C], F32, name="identity")
+        make_identity(nc, identity[:])
 
-        for t in range(BLOCKS):
-            nodes = slice(t * BLOCK, (t + 1) * BLOCK)
+        gate = {}
+        for step in range(BLOCKS + LAG):
+            if step < BLOCKS:
+                t = step
+                nodes = slice(t * BLOCK, (t + 1) * BLOCK)
 
-            agg = {}
-            for d in range(D):
-                piece = d * BLOCKS + t
-                msg = work.tile([C, PIECE], F32, name="msg")
-                nc.vector.tensor_tensor(
-                    msg[:],
-                    h_f32[:].indirect(offsets[:, piece * PIECE_COLS : (piece + 1) * PIECE_COLS]),
-                    mask_pieces[d, t][:],
-                    MULT,
-                )
-                msg_pairs = msg[:].rearrange("c (j two) -> c j two", two=2)
-                half = work.tile([C, PIECE // 2], F32, name="half")
-                nc.vector.tensor_tensor(half[:], msg_pairs[:, :, 0], msg_pairs[:, :, 1], ADD)
-                half_pairs = half[:].rearrange("c (n two) -> c n two", two=2)
-                agg[d] = work.tile([C, BLOCK], BF16, name=f"agg{d}")
-                nc.vector.tensor_tensor(agg[d][:], half_pairs[:, :, 0], half_pairs[:, :, 1], ADD)
+                agg = {}
+                for d in range(D):
+                    piece = d * BLOCKS + t
+                    msg = work.tile([C, PIECE], F32, name="msg")
+                    nc.vector.tensor_tensor(
+                        msg[:],
+                        h_f32[:].indirect(offsets[:, piece * PIECE_COLS : (piece + 1) * PIECE_COLS]),
+                        mask_pieces[d, t][:],
+                        MULT,
+                    )
+                    agg[d] = work.tile([C, BLOCK], BF16, name=f"agg{d}")
+                    if d == 0:
+                        msg_by_k = msg[:].rearrange("c (n k) -> c k n", k=K)
+                        agg_f32 = psum_sums.tile([C, BLOCK], F32, name="agg_f32")
+                        for k in range(K):
+                            nc.tensor.matmul(
+                                agg_f32[:], identity[:], msg_by_k[:, k, :], start=(k == 0), stop=(k == K - 1)
+                            )
+                        nc.scalar.copy(agg[d][:], agg_f32[:])
+                    else:
+                        msg_pairs = msg[:].rearrange("c (j two) -> c j two", two=2)
+                        half = work.tile([C, PIECE // 2], F32, name="half")
+                        nc.vector.tensor_tensor(half[:], msg_pairs[:, :, 0], msg_pairs[:, :, 1], ADD)
+                        half_pairs = half[:].rearrange("c (n two) -> c n two", two=2)
+                        nc.vector.tensor_tensor(agg[d][:], half_pairs[:, :, 0], half_pairs[:, :, 1], ADD)
 
-            pre = [psum.tile([C, BLOCK], F32, name=f"pre{q}") for q in range(Q)]
-            for q in range(Q):
-                gate_cols = slice(q * C, (q + 1) * C)
-                nc.tensor.matmul(pre[q][:], u_bf[:, gate_cols], h_bf[:, nodes], start=True, stop=False)
-            for d in range(D):
-                for q in range(Q):
-                    gate_cols = slice(q * C, (q + 1) * C)
+                in_order_of_use = (GATE_F, GATE_I, GATE_Z, GATE_O)
+                pre = {q: psum.tile([C, BLOCK], F32, name=f"pre{q}") for q in in_order_of_use}
+                for q in in_order_of_use:
                     nc.tensor.matmul(
-                        pre[q][:], w_bf[:, d, gate_cols], agg[d][:], start=False, stop=(d == D - 1)
+                        pre[q][:], u_bf[:, q * C : (q + 1) * C], h_bf[:, nodes], start=True, stop=False
+                    )
+                for d in range(D):
+                    for q in in_order_of_use:
+                        nc.tensor.matmul(
+                            pre[q][:],
+                            w_bf[:, d, q * C : (q + 1) * C],
+                            agg[d][:],
+                            start=False,
+                            stop=(d == D - 1),
+                        )
+
+                for q in in_order_of_use:
+                    gate[t, q] = gates.tile([C, BLOCK], F32, name=f"gate{q}")
+                    nc.scalar.activation(
+                        gate[t, q][:],
+                        pre[q][:],
+                        TANH if q == GATE_Z else SIGMOID,
+                        bias=bias[:, q : q + 1],
                     )
 
-            gate = []
-            for q in range(Q):
-                gate.append(work.tile([C, BLOCK], F32, name=f"gate{q}"))
-                nc.scalar.activation(
-                    gate[q][:], pre[q][:], TANH if q == Q - 1 else SIGMOID, bias=bias[:, q : q + 1]
-                )
-            gate_i, gate_o, gate_f, cand = gate
-            kept = work.tile([C, BLOCK], F32, name="kept")
-            nc.vector.tensor_tensor(kept[:], gate_f[:], cell_f32[:, nodes], MULT)
-            fresh = work.tile([C, BLOCK], F32, name="fresh")
-            nc.vector.tensor_tensor(fresh[:], gate_i[:], cand[:], MULT)
-            cnew = work.tile([C, BLOCK], F32, name="cnew")
-            nc.vector.tensor_tensor(cnew[:], kept[:], fresh[:], ADD)
-            squashed = work.tile([C, BLOCK], F32, name="squashed")
-            nc.scalar.activation(squashed[:], cnew[:], TANH)
-            result = work.tile([C, BLOCK], F32, name="result")
-            nc.vector.tensor_tensor(result[:], gate_o[:], squashed[:], MULT)
-            nc.sync.dma_start(out[:, nodes], result[:])
+            if step >= LAG:
+                t = step - LAG
+                nodes = slice(t * BLOCK, (t + 1) * BLOCK)
+                kept = work.tile([C, BLOCK], F32, name="kept")
+                nc.vector.tensor_tensor(kept[:], gate[t, GATE_F][:], cell_f32[:, nodes], MULT)
+                fresh = work.tile([C, BLOCK], F32, name="fresh")
+                nc.vector.tensor_tensor(fresh[:], gate[t, GATE_I][:], gate[t, GATE_Z][:], MULT)
+                cnew = work.tile([C, BLOCK], F32, name="cnew")
+                nc.vector.tensor_tensor(cnew[:], kept[:], fresh[:], ADD)
+                squashed = work.tile([C, BLOCK], F32, name="squashed")
+                nc.scalar.activation(squashed[:], cnew[:], TANH)
+                result = work.tile([C, BLOCK], F32, name="result")
+                nc.vector.tensor_tensor(result[:], gate[t, GATE_O][:], squashed[:], MULT)
+                nc.sync.dma_start(out[:, nodes], result[:])

@@ -18,7 +18,7 @@ BLOCK = 256
 BLOCKS = S // BLOCK
 PIECE = BLOCK * K
 PIECE_COLS = PIECE // 16
-LAG = 1
+STAGES = 3
 
 FLOPS = 2 * (D * C + C) * (Q * C) * S
 
@@ -28,7 +28,7 @@ def tile_gslstm_kernel(tc, h, cell, mask, w, u, b, offs, out):
     with (
         tc.tile_pool(name="held", bufs=1) as held,
         tc.tile_pool(name="work", bufs=3) as work,
-        tc.tile_pool(name="gates", bufs=LAG + 1) as gates,
+        tc.tile_pool(name="gates", bufs=STAGES) as gates,
         tc.psum_pool(name="psum", bufs=1) as psum,
         tc.psum_pool(name="psum_sums", bufs=2) as psum_sums,
     ):
@@ -60,7 +60,8 @@ def tile_gslstm_kernel(tc, h, cell, mask, w, u, b, offs, out):
         make_identity(nc, identity[:])
 
         gate = {}
-        for step in range(BLOCKS + LAG):
+        squashed = {}
+        for step in range(BLOCKS + STAGES - 1):
             if step < BLOCKS:
                 t = step
                 nodes = slice(t * BLOCK, (t + 1) * BLOCK)
@@ -116,8 +117,8 @@ def tile_gslstm_kernel(tc, h, cell, mask, w, u, b, offs, out):
                         bias=bias[:, q : q + 1],
                     )
 
-            if step >= LAG:
-                t = step - LAG
+            if 0 <= step - 1 < BLOCKS:
+                t = step - 1
                 nodes = slice(t * BLOCK, (t + 1) * BLOCK)
                 kept = work.tile([C, BLOCK], F32, name="kept")
                 nc.vector.tensor_tensor(kept[:], gate[t, GATE_F][:], cell_f32[:, nodes], MULT)
@@ -125,8 +126,12 @@ def tile_gslstm_kernel(tc, h, cell, mask, w, u, b, offs, out):
                 nc.vector.tensor_tensor(fresh[:], gate[t, GATE_I][:], gate[t, GATE_Z][:], MULT)
                 cnew = work.tile([C, BLOCK], F32, name="cnew")
                 nc.vector.tensor_tensor(cnew[:], kept[:], fresh[:], ADD)
-                squashed = work.tile([C, BLOCK], F32, name="squashed")
-                nc.scalar.activation(squashed[:], cnew[:], TANH)
+                squashed[t] = work.tile([C, BLOCK], F32, name="squashed")
+                nc.scalar.activation(squashed[t][:], cnew[:], TANH)
+
+            if 0 <= step - 2 < BLOCKS:
+                t = step - 2
+                nodes = slice(t * BLOCK, (t + 1) * BLOCK)
                 result = work.tile([C, BLOCK], F32, name="result")
-                nc.vector.tensor_tensor(result[:], gate[t, GATE_O][:], squashed[:], MULT)
+                nc.vector.tensor_tensor(result[:], gate[t, GATE_O][:], squashed[t][:], MULT)
                 nc.sync.dma_start(out[:, nodes], result[:])

@@ -18,7 +18,6 @@ BLOCK = 256
 BLOCKS = S // BLOCK
 PIECE = BLOCK * K
 PIECE_COLS = PIECE // 16
-STAGES = 3
 
 FLOPS = 2 * (D * C + C) * (Q * C) * S
 
@@ -28,7 +27,6 @@ def tile_gslstm_kernel(tc, h, cell, mask, w, u, b, offs, out):
     with (
         tc.tile_pool(name="held", bufs=1) as held,
         tc.tile_pool(name="work", bufs=3) as work,
-        tc.tile_pool(name="gates", bufs=STAGES) as gates,
         tc.psum_pool(name="psum", bufs=1) as psum,
         tc.psum_pool(name="psum_sums", bufs=2) as psum_sums,
     ):
@@ -36,102 +34,83 @@ def tile_gslstm_kernel(tc, h, cell, mask, w, u, b, offs, out):
         nc.sync.dma_start(offsets[:], offs)
         h_f32 = held.tile([C, S], F32, name="h_f32")
         nc.scalar.dma_start(h_f32[:], h)
+        bias = held.tile([C, Q], F32, name="bias")
+        with nc.allow_non_contiguous_dma(reason="512 biases, one to a partition and gate"):
+            nc.scalar.dma_start(bias[:], b.rearrange("(q m) one -> m (q one)", q=Q))
 
+        u_bf = held.tile([C, Q * C], BF16, name="u_bf")
+        w_bf = held.tile([C, D, Q * C], BF16, name="w_bf")
+        cell_f32 = held.tile([C, S], F32, name="cell_f32")
         mask_pieces = {}
         for t in range(BLOCKS):
             for d in range(D):
                 first = (d * S + t * BLOCK) * K
                 mask_pieces[d, t] = held.tile([C, PIECE], F32, name=f"mask_{d}_{t}")
                 nc.sync.dma_start(mask_pieces[d, t][:], mask[:, first : first + PIECE])
-
-        u_bf = held.tile([C, Q * C], BF16, name="u_bf")
-        nc.scalar.dma_start(u_bf[:], u)
-        w_bf = held.tile([C, D, Q * C], BF16, name="w_bf")
-        nc.scalar.dma_start(w_bf[:], w.rearrange("(d c) m -> c d m", d=D))
-        cell_f32 = held.tile([C, S], F32, name="cell_f32")
-        nc.scalar.dma_start(cell_f32[:], cell)
-        bias = held.tile([C, Q], F32, name="bias")
-        with nc.allow_non_contiguous_dma(reason="512 biases, one to a partition and gate"):
-            nc.scalar.dma_start(bias[:], b.rearrange("(q m) one -> m (q one)", q=Q))
+            if t == 0:
+                nc.sync.dma_start(u_bf[:], u)
+                nc.sync.dma_start(w_bf[:], w.rearrange("(d c) m -> c d m", d=D))
+        nc.sync.dma_start(cell_f32[:], cell)
 
         h_bf = held.tile([C, S], BF16, name="h_bf")
         nc.scalar.copy(h_bf[:], h_f32[:])
         identity = held.tile([C, C], F32, name="identity")
         make_identity(nc, identity[:])
 
-        gate = {}
-        squashed = {}
-        for step in range(BLOCKS + STAGES - 1):
-            if step < BLOCKS:
-                t = step
-                nodes = slice(t * BLOCK, (t + 1) * BLOCK)
+        in_order_of_use = (GATE_F, GATE_I, GATE_Z, GATE_O)
+        gate = {q: held.tile([C, S], F32, name=f"gate{q}") for q in in_order_of_use}
+        for t in range(BLOCKS):
+            nodes = slice(t * BLOCK, (t + 1) * BLOCK)
 
-                agg = {}
-                for d in range(D):
-                    piece = d * BLOCKS + t
-                    msg = work.tile([C, PIECE], F32, name="msg")
-                    nc.vector.tensor_tensor(
-                        msg[:],
-                        h_f32[:].indirect(offsets[:, piece * PIECE_COLS : (piece + 1) * PIECE_COLS]),
-                        mask_pieces[d, t][:],
-                        MULT,
-                    )
-                    agg[d] = work.tile([C, BLOCK], BF16, name=f"agg{d}")
-                    if d == 0:
-                        msg_by_k = msg[:].rearrange("c (n k) -> c k n", k=K)
-                        agg_f32 = psum_sums.tile([C, BLOCK], F32, name="agg_f32")
-                        for k in range(K):
-                            nc.tensor.matmul(
-                                agg_f32[:], identity[:], msg_by_k[:, k, :], start=(k == 0), stop=(k == K - 1)
-                            )
-                        nc.scalar.copy(agg[d][:], agg_f32[:])
-                    else:
-                        msg_pairs = msg[:].rearrange("c (j two) -> c j two", two=2)
-                        half = work.tile([C, PIECE // 2], F32, name="half")
-                        nc.vector.tensor_tensor(half[:], msg_pairs[:, :, 0], msg_pairs[:, :, 1], ADD)
-                        half_pairs = half[:].rearrange("c (n two) -> c n two", two=2)
-                        nc.vector.tensor_tensor(agg[d][:], half_pairs[:, :, 0], half_pairs[:, :, 1], ADD)
+            agg = {}
+            for d in range(D):
+                piece = d * BLOCKS + t
+                msg = held.tile([C, BLOCK, K], F32, name=f"msg_{d}_{t}")
+                nc.vector.tensor_tensor(
+                    msg[:].rearrange("c n k -> c (n k)"),
+                    h_f32[:].indirect(offsets[:, piece * PIECE_COLS : (piece + 1) * PIECE_COLS]),
+                    mask_pieces[d, t][:],
+                    MULT,
+                )
+                agg[d] = work.tile([C, BLOCK], BF16, name=f"agg{d}")
+                if d == 0:
+                    agg_f32 = psum_sums.tile([C, BLOCK], F32, name="agg_f32")
+                    for k in range(K):
+                        nc.tensor.matmul(
+                            agg_f32[:], identity[:], msg[:, :, k], start=(k == 0), stop=(k == K - 1)
+                        )
+                    nc.scalar.copy(agg[d][:], agg_f32[:])
+                else:
+                    with nc.allow_low_precision(reason="summed in float32, rounded once to bfloat16"):
+                        nc.vector.tensor_reduce(agg[d][:], msg[:], mybir.AxisListType.X, ADD)
 
-                in_order_of_use = (GATE_F, GATE_I, GATE_Z, GATE_O)
-                pre = {q: psum.tile([C, BLOCK], F32, name=f"pre{q}") for q in in_order_of_use}
+            pre = {q: psum.tile([C, BLOCK], F32, name=f"pre{q}") for q in in_order_of_use}
+            for q in in_order_of_use:
+                nc.tensor.matmul(
+                    pre[q][:], u_bf[:, q * C : (q + 1) * C], h_bf[:, nodes], start=True, stop=False
+                )
+            for d in range(D):
                 for q in in_order_of_use:
                     nc.tensor.matmul(
-                        pre[q][:], u_bf[:, q * C : (q + 1) * C], h_bf[:, nodes], start=True, stop=False
-                    )
-                for d in range(D):
-                    for q in in_order_of_use:
-                        nc.tensor.matmul(
-                            pre[q][:],
-                            w_bf[:, d, q * C : (q + 1) * C],
-                            agg[d][:],
-                            start=False,
-                            stop=(d == D - 1),
-                        )
-
-                for q in in_order_of_use:
-                    gate[t, q] = gates.tile([C, BLOCK], F32, name=f"gate{q}")
-                    nc.scalar.activation(
-                        gate[t, q][:],
-                        pre[q][:],
-                        TANH if q == GATE_Z else SIGMOID,
-                        bias=bias[:, q : q + 1],
+                        pre[q][:], w_bf[:, d, q * C : (q + 1) * C], agg[d][:], start=False, stop=(d == D - 1)
                     )
 
-            if 0 <= step - 1 < BLOCKS:
-                t = step - 1
-                nodes = slice(t * BLOCK, (t + 1) * BLOCK)
-                kept = work.tile([C, BLOCK], F32, name="kept")
-                nc.vector.tensor_tensor(kept[:], gate[t, GATE_F][:], cell_f32[:, nodes], MULT)
-                fresh = work.tile([C, BLOCK], F32, name="fresh")
-                nc.vector.tensor_tensor(fresh[:], gate[t, GATE_I][:], gate[t, GATE_Z][:], MULT)
-                cnew = work.tile([C, BLOCK], F32, name="cnew")
-                nc.vector.tensor_tensor(cnew[:], kept[:], fresh[:], ADD)
-                squashed[t] = work.tile([C, BLOCK], F32, name="squashed")
-                nc.scalar.activation(squashed[t][:], cnew[:], TANH)
+            for q in in_order_of_use:
+                nc.scalar.activation(
+                    gate[q][:, nodes], pre[q][:], TANH if q == GATE_Z else SIGMOID, bias=bias[:, q : q + 1]
+                )
 
-            if 0 <= step - 2 < BLOCKS:
-                t = step - 2
-                nodes = slice(t * BLOCK, (t + 1) * BLOCK)
-                result = work.tile([C, BLOCK], F32, name="result")
-                nc.vector.tensor_tensor(result[:], gate[t, GATE_O][:], squashed[t][:], MULT)
-                nc.sync.dma_start(out[:, nodes], result[:])
+        groups = (slice(0, S - BLOCK), slice(S - BLOCK, S))
+        kept = held.tile([C, S], F32, name="kept")
+        fresh = held.tile([C, S], F32, name="fresh")
+        cnew = held.tile([C, S], F32, name="cnew")
+        squashed = held.tile([C, S], F32, name="squashed")
+        result = held.tile([C, S], F32, name="result")
+        for nodes in groups:
+            nc.vector.tensor_tensor(kept[:, nodes], gate[GATE_F][:, nodes], cell_f32[:, nodes], MULT)
+            nc.vector.tensor_tensor(fresh[:, nodes], gate[GATE_I][:, nodes], gate[GATE_Z][:, nodes], MULT)
+            nc.vector.tensor_tensor(cnew[:, nodes], kept[:, nodes], fresh[:, nodes], ADD)
+            nc.scalar.activation(squashed[:, nodes], cnew[:, nodes], TANH)
+        for nodes in groups:
+            nc.vector.tensor_tensor(result[:, nodes], gate[GATE_O][:, nodes], squashed[:, nodes], MULT)
+            nc.sync.dma_start(out[:, nodes], result[:, nodes])

@@ -81,8 +81,9 @@ def tile_gslstm_kernel(tc, h, cell, mask, w, u, b, offs, out):
                         )
                     nc.scalar.copy(agg[d][:], agg_f32[:])
                 else:
-                    with nc.allow_low_precision(reason="summed in float32, rounded once to bfloat16"):
-                        nc.vector.tensor_reduce(agg[d][:], msg[:], mybir.AxisListType.X, ADD)
+                    pairs = work.tile([C, BLOCK, K // 2], F32, name="pairs")
+                    nc.vector.tensor_tensor(pairs[:], msg[:, :, 0:2], msg[:, :, 2:4], ADD)
+                    nc.vector.tensor_tensor(agg[d][:], pairs[:, :, 0], pairs[:, :, 1], ADD)
 
             pre = {q: psum.tile([C, BLOCK], F32, name=f"pre{q}") for q in in_order_of_use}
             for q in in_order_of_use:

@@ -1,5 +1,4 @@
 import concourse.mybir as mybir
-from concourse.masks import make_identity
 
 F32, BF16, U16 = mybir.dt.float32, mybir.dt.bfloat16, mybir.dt.uint16
 MULT, ADD = mybir.AluOpType.mult, mybir.AluOpType.add
@@ -27,8 +26,7 @@ def tile_gslstm_kernel(tc, h, cell, mask, w, u, b, offs, out):
     with (
         tc.tile_pool(name="held", bufs=1) as held,
         tc.tile_pool(name="work", bufs=3) as work,
-        tc.psum_pool(name="psum", bufs=1) as psum,
-        tc.psum_pool(name="psum_sums", bufs=2) as psum_sums,
+        tc.psum_pool(name="psum", bufs=2) as psum,
     ):
         offsets = held.tile([C, N // 16], U16, name="offsets")
         nc.sync.dma_start(offsets[:], offs)
@@ -54,8 +52,6 @@ def tile_gslstm_kernel(tc, h, cell, mask, w, u, b, offs, out):
 
         h_bf = held.tile([C, S], BF16, name="h_bf")
         nc.scalar.copy(h_bf[:], h_f32[:])
-        identity = held.tile([C, C], F32, name="identity")
-        make_identity(nc, identity[:])
 
         in_order_of_use = (GATE_F, GATE_I, GATE_Z, GATE_O)
         gate = {q: held.tile([C, S], F32, name=f"gate{q}") for q in in_order_of_use}
@@ -65,7 +61,7 @@ def tile_gslstm_kernel(tc, h, cell, mask, w, u, b, offs, out):
             agg = {}
             for d in range(D):
                 piece = d * BLOCKS + t
-                msg = held.tile([C, BLOCK, K], F32, name=f"msg_{d}_{t}")
+                msg = work.tile([C, BLOCK, K], F32, name="msg")
                 nc.vector.tensor_tensor(
                     msg[:].rearrange("c n k -> c (n k)"),
                     h_f32[:].indirect(offsets[:, piece * PIECE_COLS : (piece + 1) * PIECE_COLS]),
@@ -73,17 +69,8 @@ def tile_gslstm_kernel(tc, h, cell, mask, w, u, b, offs, out):
                     MULT,
                 )
                 agg[d] = work.tile([C, BLOCK], BF16, name=f"agg{d}")
-                if d == 0:
-                    agg_f32 = psum_sums.tile([C, BLOCK], F32, name="agg_f32")
-                    for k in range(K):
-                        nc.tensor.matmul(
-                            agg_f32[:], identity[:], msg[:, :, k], start=(k == 0), stop=(k == K - 1)
-                        )
-                    nc.scalar.copy(agg[d][:], agg_f32[:])
-                else:
-                    pairs = work.tile([C, BLOCK, K // 2], F32, name="pairs")
-                    nc.vector.tensor_tensor(pairs[:], msg[:, :, 0:2], msg[:, :, 2:4], ADD)
-                    nc.vector.tensor_tensor(agg[d][:], pairs[:, :, 0], pairs[:, :, 1], ADD)
+                with nc.allow_low_precision(reason="summed in float32, rounded once to bfloat16"):
+                    nc.vector.tensor_reduce(agg[d][:], msg[:], mybir.AxisListType.X, ADD)
 
             pre = {q: psum.tile([C, BLOCK], F32, name=f"pre{q}") for q in in_order_of_use}
             for q in in_order_of_use:

@@ -1,4 +1,5 @@
 import concourse.mybir as mybir
+from concourse.masks import make_identity
 
 F32, BF16, U16 = mybir.dt.float32, mybir.dt.bfloat16, mybir.dt.uint16
 MULT, ADD = mybir.AluOpType.mult, mybir.AluOpType.add
@@ -18,6 +19,8 @@ BLOCKS = S // BLOCK
 PIECE = BLOCK * K
 PIECE_COLS = PIECE // 16
 
+TENSOR_NODES = (192, 0)
+
 FLOPS = 2 * (D * C + C) * (Q * C) * S
 
 
@@ -26,7 +29,8 @@ def tile_gslstm_kernel(tc, h, cell, mask, w, u, b, offs, out):
     with (
         tc.tile_pool(name="held", bufs=1) as held,
         tc.tile_pool(name="work", bufs=3) as work,
-        tc.psum_pool(name="psum", bufs=2) as psum,
+        tc.psum_pool(name="psum", bufs=1) as psum,
+        tc.psum_pool(name="psum_sums", bufs=2) as psum_sums,
     ):
         offsets = held.tile([C, N // 16], U16, name="offsets")
         nc.sync.dma_start(offsets[:], offs)
@@ -52,6 +56,8 @@ def tile_gslstm_kernel(tc, h, cell, mask, w, u, b, offs, out):
 
         h_bf = held.tile([C, S], BF16, name="h_bf")
         nc.scalar.copy(h_bf[:], h_f32[:])
+        identity = held.tile([C, C], F32, name="identity")
+        make_identity(nc, identity[:])
 
         in_order_of_use = (GATE_F, GATE_I, GATE_Z, GATE_O)
         gate = {q: held.tile([C, S], F32, name=f"gate{q}") for q in in_order_of_use}
@@ -61,7 +67,7 @@ def tile_gslstm_kernel(tc, h, cell, mask, w, u, b, offs, out):
             agg = {}
             for d in range(D):
                 piece = d * BLOCKS + t
-                msg = work.tile([C, BLOCK, K], F32, name="msg")
+                msg = held.tile([C, BLOCK, K], F32, name=f"msg_{d}_{t}")
                 nc.vector.tensor_tensor(
                     msg[:].rearrange("c n k -> c (n k)"),
                     h_f32[:].indirect(offsets[:, piece * PIECE_COLS : (piece + 1) * PIECE_COLS]),
@@ -69,8 +75,16 @@ def tile_gslstm_kernel(tc, h, cell, mask, w, u, b, offs, out):
                     MULT,
                 )
                 agg[d] = work.tile([C, BLOCK], BF16, name=f"agg{d}")
+                share = TENSOR_NODES[d]
+                if share > 0:
+                    agg_f32 = psum_sums.tile([C, share], F32, name="agg_f32")
+                    for k in range(K):
+                        nc.tensor.matmul(
+                            agg_f32[:], identity[:], msg[:, :share, k], start=(k == 0), stop=(k == K - 1)
+                        )
+                    nc.scalar.copy(agg[d][:, :share], agg_f32[:])
                 with nc.allow_low_precision(reason="summed in float32, rounded once to bfloat16"):
-                    nc.vector.tensor_reduce(agg[d][:], msg[:], mybir.AxisListType.X, ADD)
+                    nc.vector.tensor_reduce(agg[d][:, share:], msg[:, share:, :], mybir.AxisListType.X, ADD)
 
             pre = {q: psum.tile([C, BLOCK], F32, name=f"pre{q}") for q in in_order_of_use}
             for q in in_order_of_use:

@@ -19,7 +19,7 @@ BLOCKS = S // BLOCK
 PIECE = BLOCK * K
 PIECE_COLS = PIECE // 16
 
-TENSOR_NODES = (192, 0)
+TENSOR_BLOCKS = BLOCKS - 1
 
 FLOPS = 2 * (D * C + C) * (Q * C) * S
 
@@ -75,16 +75,14 @@ def tile_gslstm_kernel(tc, h, cell, mask, w, u, b, offs, out):
                     MULT,
                 )
                 agg[d] = work.tile([C, BLOCK], BF16, name=f"agg{d}")
-                share = TENSOR_NODES[d]
-                if share > 0:
-                    agg_f32 = psum_sums.tile([C, share], F32, name="agg_f32")
+                if t < TENSOR_BLOCKS:
+                    agg_f32 = psum_sums.tile([C, BLOCK], F32, name="agg_f32")
                     for k in range(K):
-                        nc.tensor.matmul(
-                            agg_f32[:], identity[:], msg[:, :share, k], start=(k == 0), stop=(k == K - 1)
-                        )
-                    nc.scalar.copy(agg[d][:, :share], agg_f32[:])
-                with nc.allow_low_precision(reason="summed in float32, rounded once to bfloat16"):
-                    nc.vector.tensor_reduce(agg[d][:, share:], msg[:, share:, :], mybir.AxisListType.X, ADD)
+                        nc.tensor.matmul(agg_f32[:], identity[:], msg[:, :, k], start=(k == 0), stop=(k == K - 1))
+                    nc.scalar.copy(agg[d][:], agg_f32[:])
+                else:
+                    with nc.allow_low_precision(reason="summed in float32, rounded once to bfloat16"):
+                        nc.vector.tensor_reduce(agg[d][:], msg[:], mybir.AxisListType.X, ADD)
 
             pre = {q: psum.tile([C, BLOCK], F32, name=f"pre{q}") for q in in_order_of_use}
             for q in in_order_of_use:

@@ -76,9 +76,11 @@ def tile_gslstm_kernel(tc, h, cell, mask, w, u, b, offs, out):
                 )
                 agg[d] = work.tile([C, BLOCK], BF16, name=f"agg{d}")
                 if t < TENSOR_BLOCKS:
+                    packed = held.tile([C, K, BLOCK], F32, name=f"packed_{d}_{t}")
+                    nc.scalar.copy(packed[:], msg[:].rearrange("c n k -> c k n"))
                     agg_f32 = psum_sums.tile([C, BLOCK], F32, name="agg_f32")
                     for k in range(K):
-                        nc.tensor.matmul(agg_f32[:], identity[:], msg[:, :, k], start=(k == 0), stop=(k == K - 1))
+                        nc.tensor.matmul(agg_f32[:], identity[:], packed[:, k, :], start=(k == 0), stop=(k == K - 1))
                     nc.scalar.copy(agg[d][:], agg_f32[:])
                 else:
                     with nc.allow_low_precision(reason="summed in float32, rounded once to bfloat16"):

@@ -19,7 +19,8 @@ BLOCKS = S // BLOCK
 PIECE = BLOCK * K
 PIECE_COLS = PIECE // 16
 
-TENSOR_BLOCKS = BLOCKS - 1
+SUMMED_BY_TENSOR = ((0, 0), (0, 1), (0, 2), (0, 3), (1, 0))
+SUMMED_BY_VECTOR = ((1, 1), (1, 2), (1, 3))
 
 FLOPS = 2 * (D * C + C) * (Q * C) * S
 
@@ -30,7 +31,7 @@ def tile_gslstm_kernel(tc, h, cell, mask, w, u, b, offs, out):
         tc.tile_pool(name="held", bufs=1) as held,
         tc.tile_pool(name="work", bufs=3) as work,
         tc.psum_pool(name="psum", bufs=1) as psum,
-        tc.psum_pool(name="psum_sums", bufs=2) as psum_sums,
+        tc.psum_pool(name="psum_sums", bufs=3) as psum_sums,
     ):
         offsets = held.tile([C, N // 16], U16, name="offsets")
         nc.sync.dma_start(offsets[:], offs)
@@ -44,12 +45,11 @@ def tile_gslstm_kernel(tc, h, cell, mask, w, u, b, offs, out):
         w_bf = held.tile([C, D, Q * C], BF16, name="w_bf")
         cell_f32 = held.tile([C, S], F32, name="cell_f32")
         mask_pieces = {}
-        for t in range(BLOCKS):
-            for d in range(D):
-                first = (d * S + t * BLOCK) * K
-                mask_pieces[d, t] = held.tile([C, PIECE], F32, name=f"mask_{d}_{t}")
-                nc.sync.dma_start(mask_pieces[d, t][:], mask[:, first : first + PIECE])
-            if t == 0:
+        for d, t in SUMMED_BY_TENSOR + SUMMED_BY_VECTOR:
+            first = (d * S + t * BLOCK) * K
+            mask_pieces[d, t] = held.tile([C, PIECE], F32, name=f"mask_{d}_{t}")
+            nc.sync.dma_start(mask_pieces[d, t][:], mask[:, first : first + PIECE])
+            if (d, t) == SUMMED_BY_TENSOR[1]:
                 nc.sync.dma_start(u_bf[:], u)
                 nc.sync.dma_start(w_bf[:], w.rearrange("(d c) m -> c d m", d=D))
         nc.sync.dma_start(cell_f32[:], cell)
@@ -61,46 +61,55 @@ def tile_gslstm_kernel(tc, h, cell, mask, w, u, b, offs, out):
 
         in_order_of_use = (GATE_F, GATE_I, GATE_Z, GATE_O)
         gate = {q: held.tile([C, S], F32, name=f"gate{q}") for q in in_order_of_use}
-        for t in range(BLOCKS):
+        msg, agg, agg_f32 = {}, {}, {}
+
+        def look_up(d, t):
+            piece = d * BLOCKS + t
+            msg[d, t] = held.tile([C, BLOCK, K], F32, name=f"msg_{d}_{t}")
+            nc.vector.tensor_tensor(
+                msg[d, t][:].rearrange("c n k -> c (n k)"),
+                h_f32[:].indirect(offsets[:, piece * PIECE_COLS : (piece + 1) * PIECE_COLS]),
+                mask_pieces[d, t][:],
+                MULT,
+            )
+            agg[d, t] = held.tile([C, BLOCK], BF16, name=f"agg_{d}_{t}")
+
+        def gates(t):
             nodes = slice(t * BLOCK, (t + 1) * BLOCK)
-
-            agg = {}
-            for d in range(D):
-                piece = d * BLOCKS + t
-                msg = held.tile([C, BLOCK, K], F32, name=f"msg_{d}_{t}")
-                nc.vector.tensor_tensor(
-                    msg[:].rearrange("c n k -> c (n k)"),
-                    h_f32[:].indirect(offsets[:, piece * PIECE_COLS : (piece + 1) * PIECE_COLS]),
-                    mask_pieces[d, t][:],
-                    MULT,
-                )
-                agg[d] = work.tile([C, BLOCK], BF16, name=f"agg{d}")
-                if t < TENSOR_BLOCKS:
-                    packed = held.tile([C, K, BLOCK], F32, name=f"packed_{d}_{t}")
-                    nc.scalar.copy(packed[:], msg[:].rearrange("c n k -> c k n"))
-                    agg_f32 = psum_sums.tile([C, BLOCK], F32, name="agg_f32")
-                    for k in range(K):
-                        nc.tensor.matmul(agg_f32[:], identity[:], packed[:, k, :], start=(k == 0), stop=(k == K - 1))
-                    nc.scalar.copy(agg[d][:], agg_f32[:])
-                else:
-                    with nc.allow_low_precision(reason="summed in float32, rounded once to bfloat16"):
-                        nc.vector.tensor_reduce(agg[d][:], msg[:], mybir.AxisListType.X, ADD)
-
             pre = {q: psum.tile([C, BLOCK], F32, name=f"pre{q}") for q in in_order_of_use}
             for q in in_order_of_use:
-                nc.tensor.matmul(
-                    pre[q][:], u_bf[:, q * C : (q + 1) * C], h_bf[:, nodes], start=True, stop=False
-                )
+                nc.tensor.matmul(pre[q][:], u_bf[:, q * C : (q + 1) * C], h_bf[:, nodes], start=True, stop=False)
             for d in range(D):
                 for q in in_order_of_use:
                     nc.tensor.matmul(
-                        pre[q][:], w_bf[:, d, q * C : (q + 1) * C], agg[d][:], start=False, stop=(d == D - 1)
+                        pre[q][:], w_bf[:, d, q * C : (q + 1) * C], agg[d, t][:], start=False, stop=(d == D - 1)
                     )
-
             for q in in_order_of_use:
                 nc.scalar.activation(
                     gate[q][:, nodes], pre[q][:], TANH if q == GATE_Z else SIGMOID, bias=bias[:, q : q + 1]
                 )
+
+        before = None
+        for piece in SUMMED_BY_TENSOR:
+            look_up(*piece)
+            halves = work.tile([C, K // 2, BLOCK, 2], F32, name="halves")
+            nc.scalar.copy(halves[:], msg[piece][:].rearrange("c n (a b) -> c a n b", b=2))
+            agg_f32[piece] = psum_sums.tile([C, BLOCK], F32, name="agg_f32")
+            for k in range(K):
+                nc.tensor.matmul(
+                    agg_f32[piece][:], identity[:], halves[:, k // 2, :, k % 2], start=(k == 0), stop=(k == K - 1)
+                )
+            if before is not None:
+                nc.scalar.copy(agg[before][:], agg_f32[before][:])
+            before = piece
+        nc.scalar.copy(agg[before][:], agg_f32[before][:])
+        gates(0)
+
+        for d, t in SUMMED_BY_VECTOR:
+            look_up(d, t)
+            with nc.allow_low_precision(reason="summed in float32, rounded once to bfloat16"):
+                nc.vector.tensor_reduce(agg[d, t][:], msg[d, t][:], mybir.AxisListType.X, ADD)
+            gates(t)
 
         groups = (slice(0, S - BLOCK), slice(S - BLOCK, S))
         kept = held.tile([C, S], F32, name="kept")

@@ -17,10 +17,10 @@ N = D * S * K
 BLOCK = 256
 BLOCKS = S // BLOCK
 PIECE = BLOCK * K
-PIECE_COLS = PIECE // 16
+FIRST = 256
 
-SUMMED_BY_TENSOR = ((0, 0), (0, 1), (0, 2), (0, 3), (1, 0))
-SUMMED_BY_VECTOR = ((1, 1), (1, 2), (1, 3))
+SUMMED_BY_TENSOR = ((0, 0), (0, 1), (0, 2), (0, 3), (1, 2))
+SUMMED_BY_VECTOR = ((1, 0), (1, 1), (1, 3))
 
 FLOPS = 2 * (D * C + C) * (Q * C) * S
 
@@ -30,8 +30,7 @@ def tile_gslstm_kernel(tc, h, cell, mask, w, u, b, offs, out):
     with (
         tc.tile_pool(name="held", bufs=1) as held,
         tc.tile_pool(name="work", bufs=3) as work,
-        tc.psum_pool(name="psum", bufs=1) as psum,
-        tc.psum_pool(name="psum_sums", bufs=3) as psum_sums,
+        tc.psum_pool(name="psum_even", bufs=1) as psum_even,
     ):
         offsets = held.tile([C, N // 16], U16, name="offsets")
         nc.sync.dma_start(offsets[:], offs)
@@ -45,10 +44,13 @@ def tile_gslstm_kernel(tc, h, cell, mask, w, u, b, offs, out):
         w_bf = held.tile([C, D, Q * C], BF16, name="w_bf")
         cell_f32 = held.tile([C, S], F32, name="cell_f32")
         mask_pieces = {}
+        cuts = {}
         for d, t in SUMMED_BY_TENSOR + SUMMED_BY_VECTOR:
-            first = (d * S + t * BLOCK) * K
+            start = (d * S + t * BLOCK) * K
+            cuts[d, t] = ((0, FIRST), (FIRST, PIECE)) if (d, t) == SUMMED_BY_TENSOR[0] else ((0, PIECE),)
             mask_pieces[d, t] = held.tile([C, PIECE], F32, name=f"mask_{d}_{t}")
-            nc.sync.dma_start(mask_pieces[d, t][:], mask[:, first : first + PIECE])
+            for lo, hi in cuts[d, t]:
+                nc.sync.dma_start(mask_pieces[d, t][:, lo:hi], mask[:, start + lo : start + hi])
             if (d, t) == SUMMED_BY_TENSOR[1]:
                 nc.sync.dma_start(u_bf[:], u)
                 nc.sync.dma_start(w_bf[:], w.rearrange("(d c) m -> c d m", d=D))
@@ -62,21 +64,23 @@ def tile_gslstm_kernel(tc, h, cell, mask, w, u, b, offs, out):
         in_order_of_use = (GATE_F, GATE_I, GATE_Z, GATE_O)
         gate = {q: held.tile([C, S], F32, name=f"gate{q}") for q in in_order_of_use}
         msg, agg, agg_f32 = {}, {}, {}
+        gate_banks = [psum_even]
 
         def look_up(d, t):
-            piece = d * BLOCKS + t
+            start = (d * S + t * BLOCK) * K
             msg[d, t] = held.tile([C, BLOCK, K], F32, name=f"msg_{d}_{t}")
-            nc.vector.tensor_tensor(
-                msg[d, t][:].rearrange("c n k -> c (n k)"),
-                h_f32[:].indirect(offsets[:, piece * PIECE_COLS : (piece + 1) * PIECE_COLS]),
-                mask_pieces[d, t][:],
-                MULT,
-            )
+            for lo, hi in cuts[d, t]:
+                nc.vector.tensor_tensor(
+                    msg[d, t][:].rearrange("c n k -> c (n k)")[:, lo:hi],
+                    h_f32[:].indirect(offsets[:, (start + lo) // 16 : (start + hi) // 16]),
+                    mask_pieces[d, t][:, lo:hi],
+                    MULT,
+                )
             agg[d, t] = held.tile([C, BLOCK], BF16, name=f"agg_{d}_{t}")
 
         def gates(t):
             nodes = slice(t * BLOCK, (t + 1) * BLOCK)
-            pre = {q: psum.tile([C, BLOCK], F32, name=f"pre{q}") for q in in_order_of_use}
+            pre = {q: gate_banks[t % 2].tile([C, BLOCK], F32, name=f"pre{q}") for q in in_order_of_use}
             for q in in_order_of_use:
                 nc.tensor.matmul(pre[q][:], u_bf[:, q * C : (q + 1) * C], h_bf[:, nodes], start=True, stop=False)
             for d in range(D):
@@ -89,39 +93,41 @@ def tile_gslstm_kernel(tc, h, cell, mask, w, u, b, offs, out):
                     gate[q][:, nodes], pre[q][:], TANH if q == GATE_Z else SIGMOID, bias=bias[:, q : q + 1]
                 )
 
-        before = None
-        for piece in SUMMED_BY_TENSOR:
-            look_up(*piece)
-            halves = work.tile([C, K // 2, BLOCK, 2], F32, name="halves")
-            nc.scalar.copy(halves[:], msg[piece][:].rearrange("c n (a b) -> c a n b", b=2))
-            agg_f32[piece] = psum_sums.tile([C, BLOCK], F32, name="agg_f32")
-            for k in range(K):
-                nc.tensor.matmul(
-                    agg_f32[piece][:], identity[:], halves[:, k // 2, :, k % 2], start=(k == 0), stop=(k == K - 1)
-                )
-            if before is not None:
-                nc.scalar.copy(agg[before][:], agg_f32[before][:])
-            before = piece
-        nc.scalar.copy(agg[before][:], agg_f32[before][:])
-        gates(0)
+        with tc.psum_pool(name="psum_sums", bufs=4) as psum_sums:
+            before = None
+            for piece in SUMMED_BY_TENSOR:
+                look_up(*piece)
+                packed = work.tile([C, K, BLOCK], F32, name="packed")
+                nc.scalar.copy(packed[:], msg[piece][:].rearrange("c n k -> c k n"))
+                agg_f32[piece] = psum_sums.tile([C, BLOCK], F32, name="agg_f32")
+                for k in range(K):
+                    nc.tensor.matmul(agg_f32[piece][:], identity[:], packed[:, k, :], start=(k == 0), stop=(k == K - 1))
+                if before is not None:
+                    nc.scalar.copy(agg[before][:], agg_f32[before][:])
+                before = piece
+            nc.scalar.copy(agg[before][:], agg_f32[before][:])
 
-        for d, t in SUMMED_BY_VECTOR:
-            look_up(d, t)
-            with nc.allow_low_precision(reason="summed in float32, rounded once to bfloat16"):
-                nc.vector.tensor_reduce(agg[d, t][:], msg[d, t][:], mybir.AxisListType.X, ADD)
-            gates(t)
+        with tc.psum_pool(name="psum_odd", bufs=1) as psum_odd:
+            gate_banks.append(psum_odd)
+            for d, t in SUMMED_BY_VECTOR:
+                look_up(d, t)
+                with nc.allow_low_precision(reason="summed in float32, rounded once to bfloat16"):
+                    nc.vector.tensor_reduce(agg[d, t][:], msg[d, t][:], mybir.AxisListType.X, ADD)
+                gates(t)
+                if t == 1:
+                    gates(2)
 
-        groups = (slice(0, S - BLOCK), slice(S - BLOCK, S))
-        kept = held.tile([C, S], F32, name="kept")
-        fresh = held.tile([C, S], F32, name="fresh")
-        cnew = held.tile([C, S], F32, name="cnew")
-        squashed = held.tile([C, S], F32, name="squashed")
-        result = held.tile([C, S], F32, name="result")
-        for nodes in groups:
-            nc.vector.tensor_tensor(kept[:, nodes], gate[GATE_F][:, nodes], cell_f32[:, nodes], MULT)
-            nc.vector.tensor_tensor(fresh[:, nodes], gate[GATE_I][:, nodes], gate[GATE_Z][:, nodes], MULT)
-            nc.vector.tensor_tensor(cnew[:, nodes], kept[:, nodes], fresh[:, nodes], ADD)
-            nc.scalar.activation(squashed[:, nodes], cnew[:, nodes], TANH)
-        for nodes in groups:
-            nc.vector.tensor_tensor(result[:, nodes], gate[GATE_O][:, nodes], squashed[:, nodes], MULT)
-            nc.sync.dma_start(out[:, nodes], result[:, nodes])
+            groups = (slice(0, S - BLOCK), slice(S - BLOCK, S))
+            kept = held.tile([C, S], F32, name="kept")
+            fresh = held.tile([C, S], F32, name="fresh")
+            cnew = held.tile([C, S], F32, name="cnew")
+            squashed = held.tile([C, S], F32, name="squashed")
+            result = held.tile([C, S], F32, name="result")
+            for nodes in groups:
+                nc.vector.tensor_tensor(kept[:, nodes], gate[GATE_F][:, nodes], cell_f32[:, nodes], MULT)
+                nc.vector.tensor_tensor(fresh[:, nodes], gate[GATE_I][:, nodes], gate[GATE_Z][:, nodes], MULT)
+                nc.vector.tensor_tensor(cnew[:, nodes], kept[:, nodes], fresh[:, nodes], ADD)
+                nc.scalar.activation(squashed[:, nodes], cnew[:, nodes], TANH)
+            for nodes in groups:
+                nc.vector.tensor_tensor(result[:, nodes], gate[GATE_O][:, nodes], squashed[:, nodes], MULT)
+                nc.sync.dma_start(out[:, nodes], result[:, nodes])

@@ -97,11 +97,13 @@ def tile_gslstm_kernel(tc, h, cell, mask, w, u, b, offs, out):
             before = None
             for piece in SUMMED_BY_TENSOR:
                 look_up(*piece)
-                packed = work.tile([C, K, BLOCK], F32, name="packed")
-                nc.scalar.copy(packed[:], msg[piece][:].rearrange("c n k -> c k n"))
+                halves = work.tile([C, K // 2, BLOCK, 2], F32, name="halves")
+                nc.scalar.copy(halves[:], msg[piece][:].rearrange("c n (a b) -> c a n b", b=2))
                 agg_f32[piece] = psum_sums.tile([C, BLOCK], F32, name="agg_f32")
                 for k in range(K):
-                    nc.tensor.matmul(agg_f32[piece][:], identity[:], packed[:, k, :], start=(k == 0), stop=(k == K - 1))
+                    nc.tensor.matmul(
+                        agg_f32[piece][:], identity[:], halves[:, k // 2, :, k % 2], start=(k == 0), stop=(k == K - 1)
+                    )
                 if before is not None:
                     nc.scalar.copy(agg[before][:], agg_f32[before][:])
                 before = piece

@@ -36,9 +36,6 @@ def tile_gslstm_kernel(tc, h, cell, mask, w, u, b, offs, out):
         nc.sync.dma_start(offsets[:], offs)
         h_f32 = held.tile([C, S], F32, name="h_f32")
         nc.scalar.dma_start(h_f32[:], h)
-        bias = held.tile([C, Q], F32, name="bias")
-        with nc.allow_non_contiguous_dma(reason="512 biases, one to a partition and gate"):
-            nc.scalar.dma_start(bias[:], b.rearrange("(q m) one -> m (q one)", q=Q))
 
         u_bf = held.tile([C, Q * C], BF16, name="u_bf")
         w_bf = held.tile([C, D, Q * C], BF16, name="w_bf")
@@ -54,6 +51,9 @@ def tile_gslstm_kernel(tc, h, cell, mask, w, u, b, offs, out):
             if (d, t) == SUMMED_BY_TENSOR[1]:
                 nc.sync.dma_start(u_bf[:], u)
                 nc.sync.dma_start(w_bf[:], w.rearrange("(d c) m -> c d m", d=D))
+        bias = held.tile([C, Q], F32, name="bias")
+        with nc.allow_non_contiguous_dma(reason="512 biases, one to a partition and gate"):
+            nc.sync.dma_start(bias[:], b.rearrange("(q m) one -> m (q one)", q=Q))
         nc.sync.dma_start(cell_f32[:], cell)
 
         h_bf = held.tile([C, S], BF16, name="h_bf")

@@ -32,10 +32,10 @@ def tile_gslstm_kernel(tc, h, cell, mask, w, u, b, offs, out):
         tc.tile_pool(name="work", bufs=3) as work,
         tc.psum_pool(name="psum_even", bufs=1) as psum_even,
     ):
+        h_f32 = held.tile([C, S], F32, name="h_f32")
+        nc.sync.dma_start(h_f32[:], h)
         offsets = held.tile([C, N // 16], U16, name="offsets")
         nc.sync.dma_start(offsets[:], offs)
-        h_f32 = held.tile([C, S], F32, name="h_f32")
-        nc.scalar.dma_start(h_f32[:], h)
 
         u_bf = held.tile([C, Q * C], BF16, name="u_bf")
         w_bf = held.tile([C, D, Q * C], BF16, name="w_bf")
@@ -65,6 +65,7 @@ def tile_gslstm_kernel(tc, h, cell, mask, w, u, b, offs, out):
         gate = {q: held.tile([C, S], F32, name=f"gate{q}") for q in in_order_of_use}
         msg, agg, agg_f32 = {}, {}, {}
         gate_banks = [psum_even]
+        blocks_begun = []
 
         def look_up(d, t):
             start = (d * S + t * BLOCK) * K
@@ -80,7 +81,9 @@ def tile_gslstm_kernel(tc, h, cell, mask, w, u, b, offs, out):
 
         def gates(t):
             nodes = slice(t * BLOCK, (t + 1) * BLOCK)
-            pre = {q: gate_banks[t % 2].tile([C, BLOCK], F32, name=f"pre{q}") for q in in_order_of_use}
+            banks = gate_banks[len(blocks_begun) % 2]
+            blocks_begun.append(t)
+            pre = {q: banks.tile([C, BLOCK], F32, name=f"pre{q}") for q in in_order_of_use}
             for q in in_order_of_use:
                 nc.tensor.matmul(pre[q][:], u_bf[:, q * C : (q + 1) * C], h_bf[:, nodes], start=True, stop=False)
             for d in range(D):
@@ -111,13 +114,12 @@ def tile_gslstm_kernel(tc, h, cell, mask, w, u, b, offs, out):
 
         with tc.psum_pool(name="psum_odd", bufs=1) as psum_odd:
             gate_banks.append(psum_odd)
+            gates(2)
             for d, t in SUMMED_BY_VECTOR:
                 look_up(d, t)
                 with nc.allow_low_precision(reason="summed in float32, rounded once to bfloat16"):
                     nc.vector.tensor_reduce(agg[d, t][:], msg[d, t][:], mybir.AxisListType.X, ADD)
                 gates(t)
-                if t == 1:
-                    gates(2)
 
             groups = (slice(0, S - BLOCK), slice(S - BLOCK, S))
             kept = held.tile([C, S], F32, name="kept")

@@ -17,10 +17,14 @@ N = D * S * K
 BLOCK = 256
 BLOCKS = S // BLOCK
 PIECE = BLOCK * K
-FIRST = 256
 
-SUMMED_BY_TENSOR = ((0, 0), (0, 1), (0, 2), (0, 3), (1, 2))
-SUMMED_BY_VECTOR = ((1, 0), (1, 1), (1, 3))
+SUMMED_BY_TENSOR = ((0, 0), (0, 1), (0, 2), (0, 3), (1, 0), (1, 1))
+SUMMED_BY_VECTOR = ((1, 2), (1, 3))
+
+FIRST_PARTS = ((0, BLOCK // 2), (BLOCK // 2, BLOCK))
+FIRST_LOOK_UPS = ((0, BLOCK // 4), (BLOCK // 4, BLOCK // 2), (BLOCK // 2, BLOCK))
+
+EARLY = 2
 
 FLOPS = 2 * (D * C + C) * (Q * C) * S
 
@@ -30,7 +34,8 @@ def tile_gslstm_kernel(tc, h, cell, mask, w, u, b, offs, out):
     with (
         tc.tile_pool(name="held", bufs=1) as held,
         tc.tile_pool(name="work", bufs=3) as work,
-        tc.psum_pool(name="psum_even", bufs=1) as psum_even,
+        tc.psum_pool(name="psum_gates", bufs=EARLY) as psum_gates,
+        tc.psum_pool(name="psum_sums", bufs=4) as psum_sums,
     ):
         h_f32 = held.tile([C, S], F32, name="h_f32")
         nc.sync.dma_start(h_f32[:], h)
@@ -41,97 +46,116 @@ def tile_gslstm_kernel(tc, h, cell, mask, w, u, b, offs, out):
         w_bf = held.tile([C, D, Q * C], BF16, name="w_bf")
         cell_f32 = held.tile([C, S], F32, name="cell_f32")
         mask_pieces = {}
-        cuts = {}
+        look_ups = {}
         for d, t in SUMMED_BY_TENSOR + SUMMED_BY_VECTOR:
+            first = (d, t) == SUMMED_BY_TENSOR[0]
+            look_ups[d, t] = FIRST_LOOK_UPS if first else ((0, BLOCK),)
             start = (d * S + t * BLOCK) * K
-            cuts[d, t] = ((0, FIRST), (FIRST, PIECE)) if (d, t) == SUMMED_BY_TENSOR[0] else ((0, PIECE),)
             mask_pieces[d, t] = held.tile([C, PIECE], F32, name=f"mask_{d}_{t}")
-            for lo, hi in cuts[d, t]:
-                nc.sync.dma_start(mask_pieces[d, t][:, lo:hi], mask[:, start + lo : start + hi])
-            if (d, t) == SUMMED_BY_TENSOR[1]:
-                nc.sync.dma_start(u_bf[:], u)
+            for lo, hi in look_ups[d, t]:
+                nc.sync.dma_start(mask_pieces[d, t][:, lo * K : hi * K], mask[:, start + lo * K : start + hi * K])
+                if first and lo == 0:
+                    nc.sync.dma_start(u_bf[:], u)
+            if (d, t) == SUMMED_BY_TENSOR[3]:
                 nc.sync.dma_start(w_bf[:], w.rearrange("(d c) m -> c d m", d=D))
         bias = held.tile([C, Q], F32, name="bias")
         with nc.allow_non_contiguous_dma(reason="512 biases, one to a partition and gate"):
             nc.sync.dma_start(bias[:], b.rearrange("(q m) one -> m (q one)", q=Q))
         nc.sync.dma_start(cell_f32[:], cell)
 
+        zero = held.tile([C, 1], F32, name="zero")
+        nc.gpsimd.memset(zero[:], 0.0)
+        half = held.tile([C, 1], F32, name="half")
+        nc.scalar.activation(half[:], zero[:], SIGMOID)
+
         h_bf = held.tile([C, S], BF16, name="h_bf")
-        nc.scalar.copy(h_bf[:], h_f32[:])
+        for nodes in (slice(0, BLOCK), slice(BLOCK, S)):
+            nc.scalar.copy(h_bf[:, nodes], h_f32[:, nodes])
         identity = held.tile([C, C], F32, name="identity")
         make_identity(nc, identity[:])
 
-        in_order_of_use = (GATE_F, GATE_I, GATE_Z, GATE_O)
-        gate = {q: held.tile([C, S], F32, name=f"gate{q}") for q in in_order_of_use}
-        msg, agg, agg_f32 = {}, {}, {}
-        gate_banks = [psum_even]
-        blocks_begun = []
+        gate_pairs = ((GATE_F, GATE_I), (GATE_Z, GATE_O))
+        gate = {q: held.tile([C, S], F32, name=f"gate{q}") for pair in gate_pairs for q in pair}
+        msg, agg, pre = {}, {}, {}
 
         def look_up(d, t):
             start = (d * S + t * BLOCK) * K
             msg[d, t] = held.tile([C, BLOCK, K], F32, name=f"msg_{d}_{t}")
-            for lo, hi in cuts[d, t]:
+            for lo, hi in look_ups[d, t]:
                 nc.vector.tensor_tensor(
-                    msg[d, t][:].rearrange("c n k -> c (n k)")[:, lo:hi],
-                    h_f32[:].indirect(offsets[:, (start + lo) // 16 : (start + hi) // 16]),
-                    mask_pieces[d, t][:, lo:hi],
+                    msg[d, t][:].rearrange("c n k -> c (n k)")[:, lo * K : hi * K],
+                    h_f32[:].indirect(offsets[:, (start + lo * K) // 16 : (start + hi * K) // 16]),
+                    mask_pieces[d, t][:, lo * K : hi * K],
                     MULT,
                 )
             agg[d, t] = held.tile([C, BLOCK], BF16, name=f"agg_{d}_{t}")
 
-        def gates(t):
+        def gates_of_h(t):
             nodes = slice(t * BLOCK, (t + 1) * BLOCK)
-            banks = gate_banks[len(blocks_begun) % 2]
-            blocks_begun.append(t)
-            pre = {q: banks.tile([C, BLOCK], F32, name=f"pre{q}") for q in in_order_of_use}
-            for q in in_order_of_use:
-                nc.tensor.matmul(pre[q][:], u_bf[:, q * C : (q + 1) * C], h_bf[:, nodes], start=True, stop=False)
-            for d in range(D):
-                for q in in_order_of_use:
+            for p, pair in enumerate(gate_pairs):
+                pre[t, p] = psum_gates.tile([C, 2, BLOCK], F32, name=f"pre{p}")
+                for i, q in enumerate(pair):
                     nc.tensor.matmul(
-                        pre[q][:], w_bf[:, d, q * C : (q + 1) * C], agg[d, t][:], start=False, stop=(d == D - 1)
+                        pre[t, p][:, i, :], u_bf[:, q * C : (q + 1) * C], h_bf[:, nodes], start=(i == 0), stop=False
                     )
-            for q in in_order_of_use:
-                nc.scalar.activation(
-                    gate[q][:, nodes], pre[q][:], TANH if q == GATE_Z else SIGMOID, bias=bias[:, q : q + 1]
-                )
 
-        with tc.psum_pool(name="psum_sums", bufs=4) as psum_sums:
-            before = None
-            for piece in SUMMED_BY_TENSOR:
-                look_up(*piece)
-                halves = work.tile([C, K // 2, BLOCK, 2], F32, name="halves")
-                nc.scalar.copy(halves[:], msg[piece][:].rearrange("c n (a b) -> c a n b", b=2))
-                agg_f32[piece] = psum_sums.tile([C, BLOCK], F32, name="agg_f32")
+        def gates_of_sums(t):
+            nodes = slice(t * BLOCK, (t + 1) * BLOCK)
+            for d in range(D):
+                for p, pair in enumerate(gate_pairs):
+                    for i, q in enumerate(pair):
+                        nc.tensor.matmul(
+                            pre[t, p][:, i, :],
+                            w_bf[:, d, q * C : (q + 1) * C],
+                            agg[d, t][:],
+                            start=False,
+                            stop=(d == D - 1 and i == 1),
+                        )
+            for p, pair in enumerate(gate_pairs):
+                for i, q in enumerate(pair):
+                    nc.scalar.activation(
+                        gate[q][:, nodes], pre[t, p][:, i, :], TANH if q == GATE_Z else SIGMOID, bias=bias[:, q : q + 1]
+                    )
+
+        for t in range(EARLY):
+            gates_of_h(t)
+
+        before = None
+        for piece in SUMMED_BY_TENSOR:
+            look_up(*piece)
+            agg_f32 = psum_sums.tile([C, BLOCK], F32, name="agg_f32")
+            for lo, hi in FIRST_PARTS if before is None else ((0, BLOCK),):
+                halves = work.tile([C, K // 2, hi - lo, 2], F32, name="halves")
+                nc.scalar.copy(halves[:], msg[piece][:, lo:hi, :].rearrange("c n (a b) -> c a n b", b=2))
                 for k in range(K):
                     nc.tensor.matmul(
-                        agg_f32[piece][:], identity[:], halves[:, k // 2, :, k % 2], start=(k == 0), stop=(k == K - 1)
+                        agg_f32[:, lo:hi], identity[:], halves[:, k // 2, :, k % 2], start=(k == 0), stop=(k == K - 1)
                     )
-                if before is not None:
-                    nc.scalar.copy(agg[before][:], agg_f32[before][:])
-                before = piece
-            nc.scalar.copy(agg[before][:], agg_f32[before][:])
+            if before is not None:
+                nc.scalar.copy(agg[before[0]][:], before[1][:])
+            before = (piece, agg_f32)
+        nc.scalar.copy(agg[before[0]][:], before[1][:])
 
-        with tc.psum_pool(name="psum_odd", bufs=1) as psum_odd:
-            gate_banks.append(psum_odd)
-            gates(2)
-            for d, t in SUMMED_BY_VECTOR:
-                look_up(d, t)
+        for t in range(BLOCKS):
+            if (1, t) in SUMMED_BY_VECTOR:
+                look_up(1, t)
                 with nc.allow_low_precision(reason="summed in float32, rounded once to bfloat16"):
-                    nc.vector.tensor_reduce(agg[d, t][:], msg[d, t][:], mybir.AxisListType.X, ADD)
-                gates(t)
+                    nc.vector.tensor_reduce(agg[1, t][:], msg[1, t][:], mybir.AxisListType.X, ADD)
+            if t >= EARLY:
+                gates_of_h(t)
+            gates_of_sums(t)
 
-            groups = (slice(0, S - BLOCK), slice(S - BLOCK, S))
-            kept = held.tile([C, S], F32, name="kept")
-            fresh = held.tile([C, S], F32, name="fresh")
-            cnew = held.tile([C, S], F32, name="cnew")
-            squashed = held.tile([C, S], F32, name="squashed")
-            result = held.tile([C, S], F32, name="result")
-            for nodes in groups:
-                nc.vector.tensor_tensor(kept[:, nodes], gate[GATE_F][:, nodes], cell_f32[:, nodes], MULT)
-                nc.vector.tensor_tensor(fresh[:, nodes], gate[GATE_I][:, nodes], gate[GATE_Z][:, nodes], MULT)
-                nc.vector.tensor_tensor(cnew[:, nodes], kept[:, nodes], fresh[:, nodes], ADD)
-                nc.scalar.activation(squashed[:, nodes], cnew[:, nodes], TANH)
-            for nodes in groups:
-                nc.vector.tensor_tensor(result[:, nodes], gate[GATE_O][:, nodes], squashed[:, nodes], MULT)
-                nc.sync.dma_start(out[:, nodes], result[:, nodes])
+        groups = (slice(0, S - 2 * BLOCK), slice(S - 2 * BLOCK, S - BLOCK), slice(S - BLOCK, S))
+        kept = held.tile([C, S], F32, name="kept")
+        fresh = held.tile([C, S], F32, name="fresh")
+        cnew = held.tile([C, S], F32, name="cnew")
+        squashed = held.tile([C, S], F32, name="squashed")
+        result = held.tile([C, S], F32, name="result")
+        for nodes in groups:
+            nc.vector.tensor_tensor(kept[:, nodes], gate[GATE_F][:, nodes], cell_f32[:, nodes], MULT)
+            nc.vector.tensor_tensor(fresh[:, nodes], gate[GATE_I][:, nodes], gate[GATE_Z][:, nodes], MULT)
+            nc.vector.tensor_tensor(cnew[:, nodes], kept[:, nodes], fresh[:, nodes], ADD)
+            nc.scalar.activation(squashed[:, nodes], cnew[:, nodes], TANH)
+        for nodes in groups:
+            nc.vector.tensor_tensor(result[:, nodes], gate[GATE_O][:, nodes], squashed[:, nodes], MULT)
+            nc.sync.dma_start(out[:, nodes], result[:, nodes])

@@ -21,7 +21,8 @@ PIECE = BLOCK * K
 SUMMED_BY_TENSOR = ((0, 0), (0, 1), (0, 2), (0, 3), (1, 0), (1, 1))
 SUMMED_BY_VECTOR = ((1, 2), (1, 3))
 
-FIRST_PARTS = ((0, BLOCK // 2), (BLOCK // 2, BLOCK))
+PARTS = ((0, BLOCK // 2), (BLOCK // 2, BLOCK))
+
 FIRST_LOOK_UPS = ((0, BLOCK // 4), (BLOCK // 4, BLOCK // 2), (BLOCK // 2, BLOCK))
 
 EARLY = 2
@@ -124,7 +125,7 @@ def tile_gslstm_kernel(tc, h, cell, mask, w, u, b, offs, out):
         for piece in SUMMED_BY_TENSOR:
             look_up(*piece)
             agg_f32 = psum_sums.tile([C, BLOCK], F32, name="agg_f32")
-            for lo, hi in FIRST_PARTS if before is None else ((0, BLOCK),):
+            for lo, hi in PARTS:
                 halves = work.tile([C, K // 2, hi - lo, 2], F32, name="halves")
                 nc.scalar.copy(halves[:], msg[piece][:, lo:hi, :].rearrange("c n (a b) -> c a n b", b=2))
                 for k in range(K):
@@ -146,6 +147,7 @@ def tile_gslstm_kernel(tc, h, cell, mask, w, u, b, offs, out):
             gates_of_sums(t)
 
         groups = (slice(0, S - 2 * BLOCK), slice(S - 2 * BLOCK, S - BLOCK), slice(S - BLOCK, S))
+        tanh_groups = (slice(0, S - BLOCK), slice(S - BLOCK, S))
         kept = held.tile([C, S], F32, name="kept")
         fresh = held.tile([C, S], F32, name="fresh")
         cnew = held.tile([C, S], F32, name="cnew")
@@ -155,6 +157,7 @@ def tile_gslstm_kernel(tc, h, cell, mask, w, u, b, offs, out):
             nc.vector.tensor_tensor(kept[:, nodes], gate[GATE_F][:, nodes], cell_f32[:, nodes], MULT)
             nc.vector.tensor_tensor(fresh[:, nodes], gate[GATE_I][:, nodes], gate[GATE_Z][:, nodes], MULT)
             nc.vector.tensor_tensor(cnew[:, nodes], kept[:, nodes], fresh[:, nodes], ADD)
+        for nodes in tanh_groups:
             nc.scalar.activation(squashed[:, nodes], cnew[:, nodes], TANH)
         for nodes in groups:
             nc.vector.tensor_tensor(result[:, nodes], gate[GATE_O][:, nodes], squashed[:, nodes], MULT)

@@ -25,7 +25,7 @@ PARTS = ((0, BLOCK // 2), (BLOCK // 2, BLOCK))
 
 FIRST_LOOK_UPS = ((0, BLOCK // 4), (BLOCK // 4, BLOCK // 2), (BLOCK // 2, BLOCK))
 
-EARLY = 2
+EARLY = 3
 
 FLOPS = 2 * (D * C + C) * (Q * C) * S
 
@@ -36,7 +36,7 @@ def tile_gslstm_kernel(tc, h, cell, mask, w, u, b, offs, out):
         tc.tile_pool(name="held", bufs=1) as held,
         tc.tile_pool(name="work", bufs=3) as work,
         tc.psum_pool(name="psum_gates", bufs=EARLY) as psum_gates,
-        tc.psum_pool(name="psum_sums", bufs=4) as psum_sums,
+        tc.psum_pool(name="psum_sums", bufs=2) as psum_sums,
     ):
         h_f32 = held.tile([C, S], F32, name="h_f32")
         nc.sync.dma_start(h_f32[:], h)
@@ -132,8 +132,8 @@ def tile_gslstm_kernel(tc, h, cell, mask, w, u, b, offs, out):
                     nc.tensor.matmul(
                         agg_f32[:, lo:hi], identity[:], halves[:, k // 2, :, k % 2], start=(k == 0), stop=(k == K - 1)
                     )
-            if before is not None:
-                nc.scalar.copy(agg[before[0]][:], before[1][:])
+                if lo == 0 and before is not None:
+                    nc.scalar.copy(agg[before[0]][:], before[1][:])
             before = (piece, agg_f32)
         nc.scalar.copy(agg[before[0]][:], before[1][:])
 
@@ -146,19 +146,25 @@ def tile_gslstm_kernel(tc, h, cell, mask, w, u, b, offs, out):
                 gates_of_h(t)
             gates_of_sums(t)
 
-        groups = (slice(0, S - 2 * BLOCK), slice(S - 2 * BLOCK, S - BLOCK), slice(S - BLOCK, S))
-        tanh_groups = (slice(0, S - BLOCK), slice(S - BLOCK, S))
+        state_groups = (slice(0, 2 * BLOCK), slice(2 * BLOCK, 3 * BLOCK), slice(3 * BLOCK, S))
+        result_groups = (slice(0, BLOCK), slice(BLOCK, 3 * BLOCK), slice(3 * BLOCK, S))
         kept = held.tile([C, S], F32, name="kept")
         fresh = held.tile([C, S], F32, name="fresh")
         cnew = held.tile([C, S], F32, name="cnew")
         squashed = held.tile([C, S], F32, name="squashed")
         result = held.tile([C, S], F32, name="result")
-        for nodes in groups:
-            nc.vector.tensor_tensor(kept[:, nodes], gate[GATE_F][:, nodes], cell_f32[:, nodes], MULT)
-            nc.vector.tensor_tensor(fresh[:, nodes], gate[GATE_I][:, nodes], gate[GATE_Z][:, nodes], MULT)
+        for nodes in state_groups:
+            lo = nodes.start
+            if lo == 0:
+                lo = BLOCK
+                nc.gpsimd.tensor_tensor(kept[:, :lo], gate[GATE_F][:, :lo], cell_f32[:, :lo], MULT)
+                nc.gpsimd.tensor_tensor(fresh[:, :lo], gate[GATE_I][:, :lo], gate[GATE_Z][:, :lo], MULT)
+            rest = slice(lo, nodes.stop)
+            nc.vector.tensor_tensor(kept[:, rest], gate[GATE_F][:, rest], cell_f32[:, rest], MULT)
+            nc.vector.tensor_tensor(fresh[:, rest], gate[GATE_I][:, rest], gate[GATE_Z][:, rest], MULT)
             nc.vector.tensor_tensor(cnew[:, nodes], kept[:, nodes], fresh[:, nodes], ADD)
-        for nodes in tanh_groups:
+        for nodes in result_groups:
             nc.scalar.activation(squashed[:, nodes], cnew[:, nodes], TANH)
-        for nodes in groups:
+        for nodes in result_groups:
             nc.vector.tensor_tensor(result[:, nodes], gate[GATE_O][:, nodes], squashed[:, nodes], MULT)
             nc.sync.dma_start(out[:, nodes], result[:, nodes])

@@ -18,12 +18,14 @@ BLOCK = 256
 BLOCKS = S // BLOCK
 PIECE = BLOCK * K
 
-SUMMED_BY_TENSOR = ((0, 0), (0, 1), (0, 2), (0, 3), (1, 0), (1, 1))
+SUMMED_BY_TENSOR = ((0, 0), (1, 0), (0, 1), (1, 1), (0, 2), (0, 3))
 SUMMED_BY_VECTOR = ((1, 2), (1, 3))
+EARLY_GATES = ((0, 0), (1, 0))
 
 PARTS = ((0, BLOCK // 2), (BLOCK // 2, BLOCK))
 
 FIRST_LOOK_UPS = ((0, BLOCK // 4), (BLOCK // 4, BLOCK // 2), (BLOCK // 2, BLOCK))
+SECOND_LOOK_UPS = PARTS
 
 EARLY = 3
 
@@ -46,11 +48,16 @@ def tile_gslstm_kernel(tc, h, cell, mask, w, u, b, offs, out):
         u_bf = held.tile([C, Q * C], BF16, name="u_bf")
         w_bf = held.tile([C, D, Q * C], BF16, name="w_bf")
         cell_f32 = held.tile([C, S], F32, name="cell_f32")
+        bias = held.tile([C, Q], F32, name="bias")
         mask_pieces = {}
         look_ups = {}
         for d, t in SUMMED_BY_TENSOR + SUMMED_BY_VECTOR:
             first = (d, t) == SUMMED_BY_TENSOR[0]
-            look_ups[d, t] = FIRST_LOOK_UPS if first else ((0, BLOCK),)
+            look_ups[d, t] = ((0, BLOCK),)
+            if first:
+                look_ups[d, t] = FIRST_LOOK_UPS
+            if (d, t) == SUMMED_BY_TENSOR[1]:
+                look_ups[d, t] = SECOND_LOOK_UPS
             start = (d * S + t * BLOCK) * K
             mask_pieces[d, t] = held.tile([C, PIECE], F32, name=f"mask_{d}_{t}")
             for lo, hi in look_ups[d, t]:
@@ -59,15 +66,14 @@ def tile_gslstm_kernel(tc, h, cell, mask, w, u, b, offs, out):
                     nc.sync.dma_start(u_bf[:], u)
             if (d, t) == SUMMED_BY_TENSOR[3]:
                 nc.sync.dma_start(w_bf[:], w.rearrange("(d c) m -> c d m", d=D))
-        bias = held.tile([C, Q], F32, name="bias")
-        with nc.allow_non_contiguous_dma(reason="512 biases, one to a partition and gate"):
-            nc.sync.dma_start(bias[:], b.rearrange("(q m) one -> m (q one)", q=Q))
+                with nc.allow_non_contiguous_dma(reason="512 biases, one to a partition and gate"):
+                    nc.sync.dma_start(bias[:], b.rearrange("(q m) one -> m (q one)", q=Q))
         nc.sync.dma_start(cell_f32[:], cell)
 
         zero = held.tile([C, 1], F32, name="zero")
         nc.gpsimd.memset(zero[:], 0.0)
-        half = held.tile([C, 1], F32, name="half")
-        nc.scalar.activation(half[:], zero[:], SIGMOID)
+        unused = held.tile([C, 1], F32, name="unused")
+        nc.scalar.activation(unused[:], zero[:], SIGMOID)
 
         h_bf = held.tile([C, S], BF16, name="h_bf")
         for nodes in (slice(0, BLOCK), slice(BLOCK, S)):
@@ -100,18 +106,19 @@ def tile_gslstm_kernel(tc, h, cell, mask, w, u, b, offs, out):
                         pre[t, p][:, i, :], u_bf[:, q * C : (q + 1) * C], h_bf[:, nodes], start=(i == 0), stop=False
                     )
 
-        def gates_of_sums(t):
+        def gates_of_sum(d, t):
+            for p, pair in enumerate(gate_pairs):
+                for i, q in enumerate(pair):
+                    nc.tensor.matmul(
+                        pre[t, p][:, i, :],
+                        w_bf[:, d, q * C : (q + 1) * C],
+                        agg[d, t][:],
+                        start=False,
+                        stop=(d == D - 1 and i == 1),
+                    )
+
+        def gate_functions(t):
             nodes = slice(t * BLOCK, (t + 1) * BLOCK)
-            for d in range(D):
-                for p, pair in enumerate(gate_pairs):
-                    for i, q in enumerate(pair):
-                        nc.tensor.matmul(
-                            pre[t, p][:, i, :],
-                            w_bf[:, d, q * C : (q + 1) * C],
-                            agg[d, t][:],
-                            start=False,
-                            stop=(d == D - 1 and i == 1),
-                        )
             for p, pair in enumerate(gate_pairs):
                 for i, q in enumerate(pair):
                     nc.scalar.activation(
@@ -134,34 +141,41 @@ def tile_gslstm_kernel(tc, h, cell, mask, w, u, b, offs, out):
                     )
                 if lo == 0 and before is not None:
                     nc.scalar.copy(agg[before[0]][:], before[1][:])
+            if before is not None and before[0] in EARLY_GATES:
+                gates_of_sum(*before[0])
+                if before[0][0] == D - 1:
+                    gate_functions(before[0][1])
             before = (piece, agg_f32)
         nc.scalar.copy(agg[before[0]][:], before[1][:])
 
-        for t in range(BLOCKS):
-            if (1, t) in SUMMED_BY_VECTOR:
-                look_up(1, t)
-                with nc.allow_low_precision(reason="summed in float32, rounded once to bfloat16"):
-                    nc.vector.tensor_reduce(agg[1, t][:], msg[1, t][:], mybir.AxisListType.X, ADD)
-            if t >= EARLY:
-                gates_of_h(t)
-            gates_of_sums(t)
+        gates_of_sum(0, 1)
+        gates_of_sum(1, 1)
+        gate_functions(1)
+        gates_of_sum(0, 2)
+        gates_of_h(3)
 
-        state_groups = (slice(0, 2 * BLOCK), slice(2 * BLOCK, 3 * BLOCK), slice(3 * BLOCK, S))
-        result_groups = (slice(0, BLOCK), slice(BLOCK, 3 * BLOCK), slice(3 * BLOCK, S))
+        for d, t in SUMMED_BY_VECTOR:
+            look_up(d, t)
+            with nc.allow_low_precision(reason="summed in float32, rounded once to bfloat16"):
+                nc.vector.tensor_reduce(agg[d, t][:], msg[d, t][:], mybir.AxisListType.X, ADD)
+            gates_of_sum(d, t)
+            gate_functions(t)
+            if t == 2:
+                gates_of_sum(0, 3)
+
+        state_groups = (slice(0, 3 * BLOCK), slice(3 * BLOCK, S))
+        result_groups = (slice(0, 2 * BLOCK), slice(2 * BLOCK, 3 * BLOCK), slice(3 * BLOCK, S))
         kept = held.tile([C, S], F32, name="kept")
         fresh = held.tile([C, S], F32, name="fresh")
         cnew = held.tile([C, S], F32, name="cnew")
         squashed = held.tile([C, S], F32, name="squashed")
         result = held.tile([C, S], F32, name="result")
+        for t in range(BLOCKS):
+            nodes = slice(t * BLOCK, (t + 1) * BLOCK)
+            products_on = nc.gpsimd if t == 1 else nc.vector
+            products_on.tensor_tensor(kept[:, nodes], gate[GATE_F][:, nodes], cell_f32[:, nodes], MULT)
+            products_on.tensor_tensor(fresh[:, nodes], gate[GATE_I][:, nodes], gate[GATE_Z][:, nodes], MULT)
         for nodes in state_groups:
-            lo = nodes.start
-            if lo == 0:
-                lo = BLOCK
-                nc.gpsimd.tensor_tensor(kept[:, :lo], gate[GATE_F][:, :lo], cell_f32[:, :lo], MULT)
-                nc.gpsimd.tensor_tensor(fresh[:, :lo], gate[GATE_I][:, :lo], gate[GATE_Z][:, :lo], MULT)
-            rest = slice(lo, nodes.stop)
-            nc.vector.tensor_tensor(kept[:, rest], gate[GATE_F][:, rest], cell_f32[:, rest], MULT)
-            nc.vector.tensor_tensor(fresh[:, rest], gate[GATE_I][:, rest], gate[GATE_Z][:, rest], MULT)
             nc.vector.tensor_tensor(cnew[:, nodes], kept[:, nodes], fresh[:, nodes], ADD)
         for nodes in result_groups:
             nc.scalar.activation(squashed[:, nodes], cnew[:, nodes], TANH)

@@ -20,7 +20,7 @@ PIECE = BLOCK * K
 
 SUMMED_BY_TENSOR = ((0, 0), (1, 0), (0, 1), (1, 1), (0, 2), (0, 3))
 SUMMED_BY_VECTOR = ((1, 2), (1, 3))
-EARLY_GATES = ((0, 0), (1, 0))
+EARLY_GATES = ((0, 0), (1, 0), (0, 1), (1, 1))
 
 PARTS = ((0, BLOCK // 2), (BLOCK // 2, BLOCK))
 
@@ -148,9 +148,6 @@ def tile_gslstm_kernel(tc, h, cell, mask, w, u, b, offs, out):
             before = (piece, agg_f32)
         nc.scalar.copy(agg[before[0]][:], before[1][:])
 
-        gates_of_sum(0, 1)
-        gates_of_sum(1, 1)
-        gate_functions(1)
         gates_of_sum(0, 2)
         gates_of_h(3)
 

@@ -18,9 +18,8 @@ BLOCK = 256
 BLOCKS = S // BLOCK
 PIECE = BLOCK * K
 
-SUMMED_BY_TENSOR = ((0, 0), (1, 0), (0, 1), (1, 1), (0, 2), (0, 3))
+SUMMED_BY_TENSOR = ((0, 0), (0, 1), (0, 2), (0, 3), (1, 0), (1, 1))
 SUMMED_BY_VECTOR = ((1, 2), (1, 3))
-EARLY_GATES = ((0, 0), (1, 0), (0, 1), (1, 1))
 
 PARTS = ((0, BLOCK // 2), (BLOCK // 2, BLOCK))
 
@@ -66,8 +65,8 @@ def tile_gslstm_kernel(tc, h, cell, mask, w, u, b, offs, out):
                     nc.sync.dma_start(u_bf[:], u)
             if (d, t) == SUMMED_BY_TENSOR[3]:
                 nc.sync.dma_start(w_bf[:], w.rearrange("(d c) m -> c d m", d=D))
-                with nc.allow_non_contiguous_dma(reason="512 biases, one to a partition and gate"):
-                    nc.sync.dma_start(bias[:], b.rearrange("(q m) one -> m (q one)", q=Q))
+        with nc.allow_non_contiguous_dma(reason="512 biases, one to a partition and gate"):
+            nc.sync.dma_start(bias[:], b.rearrange("(q m) one -> m (q one)", q=Q))
         nc.sync.dma_start(cell_f32[:], cell)
 
         zero = held.tile([C, 1], F32, name="zero")
@@ -141,13 +140,16 @@ def tile_gslstm_kernel(tc, h, cell, mask, w, u, b, offs, out):
                     )
                 if lo == 0 and before is not None:
                     nc.scalar.copy(agg[before[0]][:], before[1][:])
-            if before is not None and before[0] in EARLY_GATES:
+            if before is not None and before[0] == SUMMED_BY_TENSOR[0]:
                 gates_of_sum(*before[0])
-                if before[0][0] == D - 1:
-                    gate_functions(before[0][1])
             before = (piece, agg_f32)
         nc.scalar.copy(agg[before[0]][:], before[1][:])
 
+        gates_of_sum(1, 0)
+        gate_functions(0)
+        gates_of_sum(0, 1)
+        gates_of_sum(1, 1)
+        gate_functions(1)
         gates_of_sum(0, 2)
         gates_of_h(3)
 
@@ -160,20 +162,20 @@ def tile_gslstm_kernel(tc, h, cell, mask, w, u, b, offs, out):
             if t == 2:
                 gates_of_sum(0, 3)
 
-        state_groups = (slice(0, 3 * BLOCK), slice(3 * BLOCK, S))
+        state_groups = ((nc.gpsimd, 0, 0), (nc.vector, 1, 2), (nc.vector, 3, 3))
         result_groups = (slice(0, 2 * BLOCK), slice(2 * BLOCK, 3 * BLOCK), slice(3 * BLOCK, S))
         kept = held.tile([C, S], F32, name="kept")
         fresh = held.tile([C, S], F32, name="fresh")
         cnew = held.tile([C, S], F32, name="cnew")
         squashed = held.tile([C, S], F32, name="squashed")
         result = held.tile([C, S], F32, name="result")
-        for t in range(BLOCKS):
-            nodes = slice(t * BLOCK, (t + 1) * BLOCK)
-            products_on = nc.gpsimd if t == 1 else nc.vector
-            products_on.tensor_tensor(kept[:, nodes], gate[GATE_F][:, nodes], cell_f32[:, nodes], MULT)
-            products_on.tensor_tensor(fresh[:, nodes], gate[GATE_I][:, nodes], gate[GATE_Z][:, nodes], MULT)
-        for nodes in state_groups:
-            nc.vector.tensor_tensor(cnew[:, nodes], kept[:, nodes], fresh[:, nodes], ADD)
+        for engine, first, last in state_groups:
+            for t in range(first, last + 1):
+                nodes = slice(t * BLOCK, (t + 1) * BLOCK)
+                engine.tensor_tensor(kept[:, nodes], gate[GATE_F][:, nodes], cell_f32[:, nodes], MULT)
+                engine.tensor_tensor(fresh[:, nodes], gate[GATE_I][:, nodes], gate[GATE_Z][:, nodes], MULT)
+            nodes = slice(first * BLOCK, (last + 1) * BLOCK)
+            engine.tensor_tensor(cnew[:, nodes], kept[:, nodes], fresh[:, nodes], ADD)
         for nodes in result_groups:
             nc.scalar.activation(squashed[:, nodes], cnew[:, nodes], TANH)
         for nodes in result_groups:

@@ -162,20 +162,21 @@ def tile_gslstm_kernel(tc, h, cell, mask, w, u, b, offs, out):
             if t == 2:
                 gates_of_sum(0, 3)
 
-        state_groups = ((nc.gpsimd, 0, 0), (nc.vector, 1, 2), (nc.vector, 3, 3))
+        state_groups = ((0, 0), (1, 2), (3, 3))
         result_groups = (slice(0, 2 * BLOCK), slice(2 * BLOCK, 3 * BLOCK), slice(3 * BLOCK, S))
         kept = held.tile([C, S], F32, name="kept")
         fresh = held.tile([C, S], F32, name="fresh")
         cnew = held.tile([C, S], F32, name="cnew")
         squashed = held.tile([C, S], F32, name="squashed")
         result = held.tile([C, S], F32, name="result")
-        for engine, first, last in state_groups:
+        for first, last in state_groups:
             for t in range(first, last + 1):
                 nodes = slice(t * BLOCK, (t + 1) * BLOCK)
-                engine.tensor_tensor(kept[:, nodes], gate[GATE_F][:, nodes], cell_f32[:, nodes], MULT)
-                engine.tensor_tensor(fresh[:, nodes], gate[GATE_I][:, nodes], gate[GATE_Z][:, nodes], MULT)
+                products_on = nc.gpsimd if t == 0 else nc.vector
+                products_on.tensor_tensor(kept[:, nodes], gate[GATE_F][:, nodes], cell_f32[:, nodes], MULT)
+                products_on.tensor_tensor(fresh[:, nodes], gate[GATE_I][:, nodes], gate[GATE_Z][:, nodes], MULT)
             nodes = slice(first * BLOCK, (last + 1) * BLOCK)
-            engine.tensor_tensor(cnew[:, nodes], kept[:, nodes], fresh[:, nodes], ADD)
+            nc.vector.tensor_tensor(cnew[:, nodes], kept[:, nodes], fresh[:, nodes], ADD)
         for nodes in result_groups:
             nc.scalar.activation(squashed[:, nodes], cnew[:, nodes], TANH)
         for nodes in result_groups:

@@ -23,7 +23,7 @@ SUMMED_BY_VECTOR = ((1, 2), (1, 3))
 
 PARTS = ((0, BLOCK // 2), (BLOCK // 2, BLOCK))
 
-FIRST_LOOK_UPS = ((0, BLOCK // 4), (BLOCK // 4, BLOCK // 2), (BLOCK // 2, BLOCK))
+FIRST_LOOK_UPS = ((0, BLOCK // 8), (BLOCK // 8, BLOCK // 2), (BLOCK // 2, BLOCK))
 SECOND_LOOK_UPS = PARTS
 
 EARLY = 3
@@ -61,7 +61,7 @@ def tile_gslstm_kernel(tc, h, cell, mask, w, u, b, offs, out):
             mask_pieces[d, t] = held.tile([C, PIECE], F32, name=f"mask_{d}_{t}")
             for lo, hi in look_ups[d, t]:
                 nc.sync.dma_start(mask_pieces[d, t][:, lo * K : hi * K], mask[:, start + lo * K : start + hi * K])
-                if first and lo == 0:
+                if first and hi == PARTS[0][1]:
                     nc.sync.dma_start(u_bf[:], u)
             if (d, t) == SUMMED_BY_TENSOR[3]:
                 nc.sync.dma_start(w_bf[:], w.rearrange("(d c) m -> c d m", d=D))
@@ -163,7 +163,7 @@ def tile_gslstm_kernel(tc, h, cell, mask, w, u, b, offs, out):
                 gates_of_sum(0, 3)
 
         state_groups = ((0, 0), (1, 2), (3, 3))
-        result_groups = (slice(0, 2 * BLOCK), slice(2 * BLOCK, 3 * BLOCK), slice(3 * BLOCK, S))
+        tanh_groups = (slice(0, 2 * BLOCK), slice(2 * BLOCK, 3 * BLOCK), slice(3 * BLOCK, S))
         kept = held.tile([C, S], F32, name="kept")
         fresh = held.tile([C, S], F32, name="fresh")
         cnew = held.tile([C, S], F32, name="cnew")
@@ -177,8 +177,9 @@ def tile_gslstm_kernel(tc, h, cell, mask, w, u, b, offs, out):
                 products_on.tensor_tensor(fresh[:, nodes], gate[GATE_I][:, nodes], gate[GATE_Z][:, nodes], MULT)
             nodes = slice(first * BLOCK, (last + 1) * BLOCK)
             nc.vector.tensor_tensor(cnew[:, nodes], kept[:, nodes], fresh[:, nodes], ADD)
-        for nodes in result_groups:
+        for nodes in tanh_groups:
             nc.scalar.activation(squashed[:, nodes], cnew[:, nodes], TANH)
-        for nodes in result_groups:
+        for t in range(BLOCKS):
+            nodes = slice(t * BLOCK, (t + 1) * BLOCK)
             nc.vector.tensor_tensor(result[:, nodes], gate[GATE_O][:, nodes], squashed[:, nodes], MULT)
             nc.sync.dma_start(out[:, nodes], result[:, nodes])

import concourse.mybir as mybir
from concourse.masks import make_identity

F32, BF16, U16 = mybir.dt.float32, mybir.dt.bfloat16, mybir.dt.uint16
MULT, ADD = mybir.AluOpType.mult, mybir.AluOpType.add
SIGMOID = mybir.ActivationFunctionType.Sigmoid
TANH = mybir.ActivationFunctionType.Tanh

C = 128
S = 1024
K = 4
D = 2
GATE_I, GATE_O, GATE_F, GATE_Z = 0, 1, 2, 3
Q = 4
N = D * S * K

BLOCK = 256
BLOCKS = S // BLOCK
PIECE = BLOCK * K

SUMMED_BY_TENSOR = ((0, 0), (0, 1), (0, 2), (0, 3), (1, 0), (1, 1))
SUMMED_BY_VECTOR = ((1, 2), (1, 3))

PARTS = ((0, BLOCK // 2), (BLOCK // 2, BLOCK))

FIRST_LOOK_UPS = ((0, BLOCK // 8), (BLOCK // 8, BLOCK // 2), (BLOCK // 2, BLOCK))
SECOND_LOOK_UPS = PARTS

EARLY = 3

FLOPS = 2 * (D * C + C) * (Q * C) * S


def tile_gslstm_kernel(tc, h, cell, mask, w, u, b, offs, out):
    nc = tc.nc
    with (
        tc.tile_pool(name="held", bufs=1) as held,
        tc.tile_pool(name="work", bufs=3) as work,
        tc.psum_pool(name="psum_gates", bufs=EARLY) as psum_gates,
        tc.psum_pool(name="psum_sums", bufs=2) as psum_sums,
    ):
        h_f32 = held.tile([C, S], F32, name="h_f32")
        nc.sync.dma_start(h_f32[:], h)
        offsets = held.tile([C, N // 16], U16, name="offsets")
        nc.sync.dma_start(offsets[:], offs)

        u_bf = held.tile([C, Q * C], BF16, name="u_bf")
        w_bf = held.tile([C, D, Q * C], BF16, name="w_bf")
        cell_f32 = held.tile([C, S], F32, name="cell_f32")
        bias = held.tile([C, Q], F32, name="bias")
        mask_pieces = {}
        look_ups = {}
        for d, t in SUMMED_BY_TENSOR + SUMMED_BY_VECTOR:
            first = (d, t) == SUMMED_BY_TENSOR[0]
            look_ups[d, t] = ((0, BLOCK),)
            if first:
                look_ups[d, t] = FIRST_LOOK_UPS
            if (d, t) == SUMMED_BY_TENSOR[1]:
                look_ups[d, t] = SECOND_LOOK_UPS
            start = (d * S + t * BLOCK) * K
            mask_pieces[d, t] = held.tile([C, PIECE], F32, name=f"mask_{d}_{t}")
            for lo, hi in look_ups[d, t]:
                nc.sync.dma_start(mask_pieces[d, t][:, lo * K : hi * K], mask[:, start + lo * K : start + hi * K])
                if first and hi == PARTS[0][1]:
                    nc.sync.dma_start(u_bf[:], u)
            if (d, t) == SUMMED_BY_TENSOR[3]:
                nc.sync.dma_start(w_bf[:], w.rearrange("(d c) m -> c d m", d=D))
        with nc.allow_non_contiguous_dma(reason="512 biases, one to a partition and gate"):
            nc.sync.dma_start(bias[:], b.rearrange("(q m) one -> m (q one)", q=Q))
        nc.sync.dma_start(cell_f32[:], cell)

        zero = held.tile([C, 1], F32, name="zero")
        nc.gpsimd.memset(zero[:], 0.0)
        unused = held.tile([C, 1], F32, name="unused")
        nc.scalar.activation(unused[:], zero[:], SIGMOID)

        h_bf = held.tile([C, S], BF16, name="h_bf")
        for nodes in (slice(0, BLOCK), slice(BLOCK, S)):
            nc.scalar.copy(h_bf[:, nodes], h_f32[:, nodes])
        identity = held.tile([C, C], F32, name="identity")
        make_identity(nc, identity[:])

        gate_pairs = ((GATE_F, GATE_I), (GATE_Z, GATE_O))
        gate = {q: held.tile([C, S], F32, name=f"gate{q}") for pair in gate_pairs for q in pair}
        msg, agg, pre = {}, {}, {}

        def look_up(d, t):
            start = (d * S + t * BLOCK) * K
            msg[d, t] = held.tile([C, BLOCK, K], F32, name=f"msg_{d}_{t}")
            for lo, hi in look_ups[d, t]:
                nc.vector.tensor_tensor(
                    msg[d, t][:].rearrange("c n k -> c (n k)")[:, lo * K : hi * K],
                    h_f32[:].indirect(offsets[:, (start + lo * K) // 16 : (start + hi * K) // 16]),
                    mask_pieces[d, t][:, lo * K : hi * K],
                    MULT,
                )
            agg[d, t] = held.tile([C, BLOCK], BF16, name=f"agg_{d}_{t}")

        def gates_of_h(t):
            nodes = slice(t * BLOCK, (t + 1) * BLOCK)
            for p, pair in enumerate(gate_pairs):
                pre[t, p] = psum_gates.tile([C, 2, BLOCK], F32, name=f"pre{p}")
                for i, q in enumerate(pair):
                    nc.tensor.matmul(
                        pre[t, p][:, i, :], u_bf[:, q * C : (q + 1) * C], h_bf[:, nodes], start=(i == 0), stop=False
                    )

        def gates_of_sum(d, t):
            for p, pair in enumerate(gate_pairs):
                for i, q in enumerate(pair):
                    nc.tensor.matmul(
                        pre[t, p][:, i, :],
                        w_bf[:, d, q * C : (q + 1) * C],
                        agg[d, t][:],
                        start=False,
                        stop=(d == D - 1 and i == 1),
                    )

        def gate_functions(t):
            nodes = slice(t * BLOCK, (t + 1) * BLOCK)
            for p, pair in enumerate(gate_pairs):
                for i, q in enumerate(pair):
                    nc.scalar.activation(
                        gate[q][:, nodes], pre[t, p][:, i, :], TANH if q == GATE_Z else SIGMOID, bias=bias[:, q : q + 1]
                    )

        for t in range(EARLY):
            gates_of_h(t)

        before = None
        for piece in SUMMED_BY_TENSOR:
            look_up(*piece)
            agg_f32 = psum_sums.tile([C, BLOCK], F32, name="agg_f32")
            for lo, hi in PARTS:
                halves = work.tile([C, K // 2, hi - lo, 2], F32, name="halves")
                nc.scalar.copy(halves[:], msg[piece][:, lo:hi, :].rearrange("c n (a b) -> c a n b", b=2))
                for k in range(K):
                    nc.tensor.matmul(
                        agg_f32[:, lo:hi], identity[:], halves[:, k // 2, :, k % 2], start=(k == 0), stop=(k == K - 1)
                    )
                if lo == 0 and before is not None:
                    nc.scalar.copy(agg[before[0]][:], before[1][:])
            if before is not None and before[0] == SUMMED_BY_TENSOR[0]:
                gates_of_sum(*before[0])
            before = (piece, agg_f32)
        nc.scalar.copy(agg[before[0]][:], before[1][:])

        gates_of_sum(1, 0)
        gate_functions(0)
        gates_of_sum(0, 1)
        gates_of_sum(1, 1)
        gate_functions(1)
        gates_of_sum(0, 2)
        gates_of_h(3)

        for d, t in SUMMED_BY_VECTOR:
            look_up(d, t)
            with nc.allow_low_precision(reason="summed in float32, rounded once to bfloat16"):
                nc.vector.tensor_reduce(agg[d, t][:], msg[d, t][:], mybir.AxisListType.X, ADD)
            gates_of_sum(d, t)
            gate_functions(t)
            if t == 2:
                gates_of_sum(0, 3)

        state_groups = ((0, 0), (1, 2), (3, 3))
        tanh_groups = (slice(0, 2 * BLOCK), slice(2 * BLOCK, 3 * BLOCK), slice(3 * BLOCK, S))
        kept = held.tile([C, S], F32, name="kept")
        fresh = held.tile([C, S], F32, name="fresh")
        cnew = held.tile([C, S], F32, name="cnew")
        squashed = held.tile([C, S], F32, name="squashed")
        result = held.tile([C, S], F32, name="result")
        for first, last in state_groups:
            for t in range(first, last + 1):
                nodes = slice(t * BLOCK, (t + 1) * BLOCK)
                products_on = nc.gpsimd if t == 0 else nc.vector
                products_on.tensor_tensor(kept[:, nodes], gate[GATE_F][:, nodes], cell_f32[:, nodes], MULT)
                products_on.tensor_tensor(fresh[:, nodes], gate[GATE_I][:, nodes], gate[GATE_Z][:, nodes], MULT)
            nodes = slice(first * BLOCK, (last + 1) * BLOCK)
            nc.vector.tensor_tensor(cnew[:, nodes], kept[:, nodes], fresh[:, nodes], ADD)
        for nodes in tanh_groups:
            nc.scalar.activation(squashed[:, nodes], cnew[:, nodes], TANH)
        for t in range(BLOCKS):
            nodes = slice(t * BLOCK, (t + 1) * BLOCK)
            nc.vector.tensor_tensor(result[:, nodes], gate[GATE_O][:, nodes], squashed[:, nodes], MULT)
            nc.sync.dma_start(out[:, nodes], result[:, nodes])
